import numpy as np
import ml_dtypes


def mxq(x, axis, fmt="e4m3"):
    dtype, down = {"e4m3": (ml_dtypes.float8_e4m3fn, 7), "e5m2": (ml_dtypes.float8_e5m2, 14)}[fmt]
    v = np.moveaxis(np.asarray(x, np.float32).astype(ml_dtypes.bfloat16).astype(np.float64), axis, -1)
    blocks = v.reshape(v.shape[:-1] + (-1, 32))
    amax = np.abs(blocks).max(-1, keepdims=True)
    byte = np.maximum(np.where(amax > 0, np.frexp(amax)[1] - 1 + 127, 0) - down, 1)
    scale = np.exp2(byte - 127.0)
    codes = (blocks / scale).astype(np.float32).astype(dtype).astype(np.float64)
    return np.moveaxis((codes * scale).reshape(v.shape), -1, axis)


WIDE = False


def mx_kscale(k):
    if not WIDE:
        return np.ones(k)
    levels = np.array([18, -18])
    if k % 512:
        return np.exp2(np.random.permutation(np.resize(levels, k // 32))).repeat(32)
    a = np.empty((k // 512, 16))
    for p in range(k // 512):
        a[p, :8] = np.random.permutation(np.resize(levels, 8))
        for g in range(8):
            far = levels[np.abs(levels - a[p, g]) >= 10]
            a[p, g + 8] = far[np.random.randint(len(far))]
    return np.exp2(a.ravel()).repeat(32)


BF16 = ml_dtypes.bfloat16


def bf(x):
    return np.asarray(x, np.float32).astype(BF16)


def f64(x):
    return np.asarray(x).astype(np.float64)


B, S, DIM, H, NOPE, ROPE_SP = 2, 512, 1024, 8, 64, 128
C = 1.0
QK_SP = NOPE + ROPE_SP
T, J = B * S, H * QK_SP


def rope(u, cos, sin):
    u1, u2 = u[..., 0::2], u[..., 1::2]
    cos, sin = cos[None, :, None, :], sin[None, :, None, :]
    return np.stack([u1 * cos - u2 * sin, u1 * sin + u2 * cos], -1).reshape(u.shape)


def rope_back(d, cos, sin):
    d1, d2 = d[..., 0::2], d[..., 1::2]
    cos, sin = cos[None, :, None, :], sin[None, :, None, :]
    return np.stack([d1 * cos + d2 * sin, d2 * cos - d1 * sin], -1).reshape(d.shape)


def setup_inputs():
    s = mx_kscale(T).reshape(B, S)
    u = mx_kscale(J)[::QK_SP]
    inv = 1.0 / (10000.0 ** (np.arange(0, ROPE_SP, 2) / ROPE_SP))
    ang = np.arange(S)[:, None] * inv[None, :]
    x0 = bf(np.random.standard_normal((B, S, DIM)))
    cos = bf(np.cos(ang))
    sin = bf(np.sin(ang))
    w0 = bf(np.random.standard_normal((J, DIM)) * 0.3 / np.sqrt(DIM))
    b = bf(np.random.standard_normal(J) * 0.1)
    g = np.random.standard_normal((B, S, H, 1 + QK_SP)) * np.exp2(np.random.randint(-6, 1, (B, S, 1, 1))) * 4.0
    g = np.concatenate([g[..., :1] * 8.0, g[..., 1:]], -1)
    q = (f64(x0).reshape(T, DIM) @ f64(w0).T + f64(b)).reshape(B, S, H, QK_SP)
    q = np.concatenate([q[..., :NOPE], rope(q[..., NOPE:], f64(cos), f64(sin))], -1)
    t = np.sqrt((q * q).sum(-1, keepdims=True) + C)
    return {"x": bf(f64(x0) * s[:, :, None]),
            "freqs_cos": cos,
            "freqs_sin": sin,
            "wq_w": bf(f64(w0) / np.repeat(u, QK_SP)[:, None]),
            "wq_b": b,
            "q_rot": np.asarray(q, np.float32),
            "t": np.asarray(t, np.float32),
            "grad_out": bf(g / s[:, :, None, None] * u[None, None, :, None])}


def reference(x, freqs_cos, freqs_sin, wq_w, wq_b, q_rot, t, grad_out):
    g = f64(grad_out)
    dr = g[..., 1:] + g[..., :1] * f64(q_rot) / f64(t)
    dpe = rope_back(dr[..., NOPE:], f64(freqs_cos), f64(freqs_sin))
    da = np.concatenate([dr[..., :NOPE], dpe], -1).reshape(T, J)
    dx = mxq(da, 1, "e5m2") @ mxq(f64(wq_w), 0, "e4m3")
    dw = mxq(da, 0, "e5m2").T @ mxq(f64(x).reshape(T, DIM), 0, "e4m3")
    return dx.reshape(B, S, DIM), dw

@@ -1,0 +1,279 @@
+from contextlib import ExitStack
+
+import concourse.mybir as mybir
+from concourse.masks import make_identity
+
+B, S, DIM, H = 2, 512, 1024, 8
+NOPE, ROPE = 64, 128
+D = NOPE + ROPE
+DG = D + 1
+T, J = B * S, H * D
+P = 128
+PACK = 4
+KP = P * PACK
+NPASS_J = J // KP
+NT = 512
+HU = 2
+WU = HU * D
+
+FLOPS = 2 * 2 * T * J * DIM
+BYTES = 2 * (T * DIM + 2 * S * 64 + J * DIM + T * H * DG) + 4 * (T * H * D + T * H + T * DIM + J * DIM)
+
+F32 = mybir.dt.float32
+BF16 = mybir.dt.bfloat16
+U32 = mybir.dt.uint32
+U8 = mybir.dt.uint8
+E4 = mybir.dt.float8_e4m3fn_x4
+E5 = mybir.dt.float8_e5m2_x4
+ADD = mybir.AluOpType.add
+MULT = mybir.AluOpType.mult
+
+UNITS = [(0, 0), (0, 2), (1, 0), (1, 2), (0, 4), (0, 6), (1, 4), (1, 6)]
+
+
+def tile_lorentzmla_pb_v_kernel(tc, x, freqs_cos, freqs_sin, wq_w, wq_b, q_rot, t, grad_out, out_0, out_1):
+    nc = tc.nc
+    with ExitStack() as ctx:
+        keep = ctx.enter_context(tc.tile_pool(name="keep", bufs=1))
+        pool = ctx.enter_context(tc.tile_pool(name="work", bufs=2))
+        psum = ctx.enter_context(tc.psum_pool(name="psum", bufs=1))
+
+        t_sb = keep.tile([P, B, PACK, H], F32, name="t_sb")
+        nc.sync.dma_start(out=t_sb[:], in_=t.rearrange("b (p j) h o -> p b j (h o)", j=PACK))
+        q_of, g_of = {}, {}
+
+        def load_g(b, h0, nh, bufs):
+            g_t = pool.tile([P, PACK, nh * DG], BF16, name="g%d" % nh, bufs=bufs)
+            src = grad_out[b].rearrange("(p j) h d -> p j (h d)", j=PACK)
+            nc.sync.dma_start(out=g_t[:], in_=src[:, :, h0 * DG:(h0 + nh) * DG])
+            for h in range(nh):
+                g_of[(b, h0 + h)] = (g_t, h * DG)
+
+        def load_q(b, h0, nh, bufs, by_slot=False):
+            q_t = pool.tile([P, PACK, nh * D], F32, name="q%d" % nh, bufs=bufs)
+            src = q_rot[b].rearrange("(p j) h d -> p j (h d)", j=PACK)[:, :, h0 * D:(h0 + nh) * D]
+            if by_slot:
+                for j in range(PACK):
+                    nc.sync.dma_start(out=q_t[:, j, :], in_=src[:, j, :])
+            else:
+                nc.sync.dma_start(out=q_t[:], in_=src)
+            for h in range(nh):
+                q_of[(b, h0 + h)] = (q_t, h * D)
+
+        raw_of = {}
+
+        def load_raw(key, src):
+            raw = pool.tile([P, PACK, DIM], BF16, name="raw", bufs=3)
+            nc.sync.dma_start(out=raw[:], in_=src.rearrange("(p j) d -> p j d", j=PACK))
+            raw_of[key] = raw
+
+        load_g(0, 0, 2, 2)
+        load_q(0, 0, 2, 2, by_slot=True)
+        cs = keep.tile([P, 2, PACK * 64], BF16, name="cs")
+        nc.sync.dma_start(out=cs[:, 0, :], in_=freqs_cos.rearrange("(p j) f -> p (j f)", j=PACK))
+        nc.sync.dma_start(out=cs[:, 1, :], in_=freqs_sin.rearrange("(p j) f -> p (j f)", j=PACK))
+        load_raw(("x", 0), x[0])
+        load_g(0, 2, 2, 2)
+        load_q(0, 2, 2, 2)
+        load_raw(("x", 1), x[1])
+        load_g(1, 0, 4, 2)
+        load_q(1, 0, 4, 2)
+        load_raw(("w", 0), wq_w[0:KP, :])
+        load_g(0, 4, 4, 2)
+        load_q(0, 4, 4, 2)
+        load_raw(("w", 1), wq_w[KP:2 * KP, :])
+        load_raw(("w", 2), wq_w[2 * KP:3 * KP, :])
+        load_g(1, 4, 4, 2)
+        load_q(1, 4, 4, 2)
+
+        ident = keep.tile([P, P], F32, name="ident")
+        make_identity(nc, ident[:])
+        ident_b = keep.tile([P, P], BF16, name="ident_b")
+        make_identity(nc, ident_b[:])
+        tab = keep.tile([P, 2, PACK * 64, 2], BF16, name="tab")
+        nc.gpsimd.tensor_scalar(out=tab[:, 0, :, :], in0=cs[:, 0, :].unsqueeze(2).to_broadcast([P, PACK * 64, 2]),
+                                scalar1=1.0, scalar2=0.0, op0=MULT, op1=ADD)
+        nc.gpsimd.tensor_scalar(out=tab[:, 1, :, 0], in0=cs[:, 1, :], scalar1=-1.0, scalar2=0.0, op0=MULT, op1=ADD)
+        nc.gpsimd.tensor_scalar(out=tab[:, 1, :, 1], in0=cs[:, 1, :], scalar1=1.0, scalar2=0.0, op0=MULT, op1=ADD)
+        tab_ps = psum.tile([P, 2, PACK * ROPE], BF16, name="tab_ps")
+        for k in range(2):
+            nc.tensor.matmul(tab_ps[:, k, :], lhsT=ident_b[:], rhs=tab[:, k, :, :].rearrange("p n e -> p (n e)"), start=True, stop=True)
+
+        rt = keep.tile([P, B, PACK, H], F32, name="rt")
+        nc.vector.reciprocal(out=rt[:], in_=t_sb[:])
+
+        xc = keep.tile([P, B, DIM], U32, name="xc", align_bytes=64)
+        xs = keep.tile([P, B, DIM], U8, name="xs", align_bytes=64)
+        wc = keep.tile([P, NPASS_J, DIM], U32, name="wc", align_bytes=64)
+        ws = keep.tile([P, NPASS_J, DIM], U8, name="ws", align_bytes=64)
+        tcd = keep.tile([P, B, J], U32, name="tcd", align_bytes=64)
+        tsc = keep.tile([P, B, J], U8, name="tsc", align_bytes=64)
+        fcd = keep.tile([P, B, NPASS_J, S], U32, name="fcd", align_bytes=64)
+        fsc = keep.tile([P, B, NPASS_J, S], U8, name="fsc", align_bytes=64)
+        da_of = [keep.tile([P, PACK, J], BF16, name="da0", align_bytes=64),
+                 keep.tile([P, PACK, J], BF16, name="da1", align_bytes=64)]
+
+        st = {}
+
+        def coef(u):
+            b, h0 = UNITS[u]
+            g_t, go = g_of[(b, h0)]
+            c = pool.tile([P, PACK, HU], F32, name="c", bufs=3)
+            g0 = g_t[:, :, go:go + HU * DG].rearrange("p j (h d) -> p j h d", d=DG)[:, :, :, 0]
+            nc.vector.tensor_tensor(out=c[:], in0=g0, in1=rt[:, b, :, h0:h0 + HU], op=MULT)
+            st[("c", u)] = c
+
+        def lift(u):
+            b, h0 = UNITS[u]
+            c = st[("c", u)]
+            dr = pool.tile([P, PACK, HU, D], F32, name="dr", bufs=3)
+            st[("dr", u)] = dr
+            for j in range(PACK):
+                for h in range(HU):
+                    q_t, qo = q_of[(b, h0 + h)]
+                    g_t, go = g_of[(b, h0 + h)]
+                    nc.vector.scalar_tensor_tensor(
+                        out=dr[:, j, h, :], in0=q_t[:, j, qo:qo + D], scalar=c[:, j, h:h + 1],
+                        in1=g_t[:, j, go + 1:go + DG], op0=MULT, op1=ADD)
+            nc.scalar.copy(out=da_of[b][:, :, h0 * D:(h0 + HU) * D].rearrange("p j (h d) -> p j h d", d=D)[:, :, :, 0:NOPE],
+                           in_=dr[:, :, :, 0:NOPE])
+
+        def products(u):
+            dr = st[("dr", u)]
+            a = pool.tile([P, PACK, HU, ROPE], F32, name="a", bufs=2)
+            st[("a", u)] = a
+
+            def table(k):
+                v = tab_ps[:, k, :].rearrange("p (j d) -> p j d", d=ROPE)
+                return v.unsqueeze(2).to_broadcast([P, PACK, HU, ROPE])
+
+            pe = dr[:, :, :, NOPE:D]
+            nc.vector.tensor_tensor(out=a[:], in0=pe, in1=table(0), op=MULT)
+            nc.vector.tensor_tensor(out=pe, in0=pe, in1=table(1), op=MULT)
+
+        def combine(u):
+            b, h0 = UNITS[u]
+            a, dr = st[("a", u)], st[("dr", u)]
+            dst = da_of[b][:, :, h0 * D:(h0 + HU) * D].rearrange("p j (h d) -> p j h d", d=D)[:, :, :, NOPE:D]
+            sw = dr[:, :, :, NOPE:D].rearrange("p j h (f e) -> p j h f e", e=2)[:, :, :, :, ::-1]
+            nc.vector.tensor_tensor(out=dst.rearrange("p j h (f e) -> p j h f e", e=2),
+                                    in0=a[:].rearrange("p j h (f e) -> p j h f e", e=2), in1=sw, op=ADD)
+
+        def interleave(u):
+            b, h0 = UNITS[u]
+            ti = pool.tile([P, WU, PACK], BF16, name="ti", bufs=3, align_bytes=64)
+            nc.gpsimd.tensor_scalar(out=ti[:], in0=da_of[b][:, :, h0 * D:(h0 + HU) * D].rearrange("p j w -> p w j"),
+                                    scalar1=1.0, scalar2=0.0, op0=MULT, op1=ADD)
+            st[("ti", u)] = ti
+
+        def token_quant(u):
+            b, h0 = UNITS[u]
+            ti = st[("ti", u)]
+            w0 = h0 * D
+            for (o, n) in ((0, 256), (256, 128)):
+                nc.vector.quantize_mx(out=tcd[:, b, w0 + o:w0 + o + n].bitcast(E5), scales=tsc[:, b, w0 + o:w0 + o + n],
+                                      in_=ti[:, o:o + n, :].rearrange("p w j -> p (w j)"))
+
+        def transposes(b, g):
+            fi = pool.tile([P, S, PACK], BF16, name="fi", bufs=3, align_bytes=64)
+            st[("fi", b, g)] = fi
+            words = fi[:].rearrange("p n t -> p (n t)").bitcast(F32)
+            for jj in range(2):
+                tr = psum.tile([P, 2, 2, P], F32, name="tr", bufs=2)
+                for k in range(2):
+                    src = da_of[b][:, 2 * jj + k, :].bitcast(F32)
+                    for v in range(2):
+                        nc.tensor.transpose(tr[:, k, v, :], src[:, 256 * g + v:256 * (g + 1):2], ident[:])
+                nc.scalar.copy(out=words[:, 512 * jj:512 * (jj + 1)].rearrange("p (k r v) -> p k r v", k=2, v=2),
+                               in_=tr[:].rearrange("p k v r -> p k r v"))
+
+        def feature_quant(b, g):
+            fi = st[("fi", b, g)]
+            nc.vector.quantize_mx(out=fcd[:, b, g, :].bitcast(E5), scales=fsc[:, b, g, :], in_=fi[:].rearrange("p n t -> p (n t)"))
+
+        pieces = [("x", 0, 0), ("x", 0, 1), ("x", 1, 0), ("x", 1, 1)] + [("w", g, n) for g in range(3) for n in range(2)]
+
+        def piece_copy(i):
+            kind, g, n = pieces[i]
+            raw = raw_of[(kind, g)]
+            s = pool.tile([P, NT, PACK], BF16, name="stage", bufs=3, align_bytes=64)
+            st[("piece", i)] = s
+            nc.scalar.copy(out=s[:].rearrange("p (c i) t -> p c t i", i=4),
+                           in_=raw[:, :, n * NT:(n + 1) * NT].rearrange("p t (c i) -> p c t i", i=4))
+
+        def piece_quant(i):
+            kind, g, n = pieces[i]
+            s = st[("piece", i)]
+            codes, scales = (xc, xs) if kind == "x" else (wc, ws)
+            nc.vector.quantize_mx(out=codes[:, g, n * NT:(n + 1) * NT].bitcast(E4), scales=scales[:, g, n * NT:(n + 1) * NT],
+                                  in_=s[:].rearrange("p n t -> p (n t)"))
+
+        evac_n = [0]
+
+        def evac(out, in_, tail):
+            if tail and evac_n[0] % 2 == 1:
+                nc.vector.tensor_copy(out=out, in_=in_)
+            else:
+                nc.scalar.copy(out=out, in_=in_)
+            evac_n[0] += 1
+
+        def dw_tile(f, tail=False):
+            o = pool.tile([P, DIM], F32, name="o", bufs=4)
+            for n in range(2):
+                acc = psum.tile([P, NT], F32, name="mm", bufs=5)
+                for b in range(B):
+                    nc.tensor.matmul_mx(out=acc[:], lhsT=tcd[:, b, f * P:(f + 1) * P].bitcast(E5), lhsT_scale=tsc[:, b, f * P:(f + 1) * P],
+                                        rhs=xc[:, b, n * NT:(n + 1) * NT].bitcast(E4), rhs_scale=xs[:, b, n * NT:(n + 1) * NT],
+                                        start=(b == 0), stop=(b == B - 1))
+                evac(o[:, n * NT:(n + 1) * NT], acc[:], tail)
+            nc.sync.dma_start(out=out_1[f * P:(f + 1) * P, :], in_=o[:])
+
+        def dx_tile(b, j, tail=False):
+            o = pool.tile([P, DIM], F32, name="o", bufs=4)
+            for n in range(2):
+                acc = psum.tile([P, NT], F32, name="mm", bufs=5)
+                for g in range(NPASS_J):
+                    nc.tensor.matmul_mx(out=acc[:], lhsT=fcd[:, b, g, j * P:(j + 1) * P].bitcast(E5), lhsT_scale=fsc[:, b, g, j * P:(j + 1) * P],
+                                        rhs=wc[:, g, n * NT:(n + 1) * NT].bitcast(E4), rhs_scale=ws[:, g, n * NT:(n + 1) * NT],
+                                        start=(g == 0), stop=(g == NPASS_J - 1))
+                evac(o[:, n * NT:(n + 1) * NT], acc[:], tail)
+            nc.sync.dma_start(out=out_0[b].rearrange("(p j) d -> p j d", j=PACK)[:, j, :], in_=o[:])
+
+        PASSES = {0: [], 2: [0], 4: [1], 6: [2]}
+        n_units = len(UNITS)
+        coef(0)
+        next_piece, quanted = 0, 0
+        for u in range(n_units + 2):
+            if u + 1 < n_units:
+                coef(u + 1)
+            if u < n_units:
+                lift(u)
+            if 0 <= u - 2:
+                b, h0 = UNITS[u - 2]
+                token_quant(u - 2)
+                for g in PASSES[h0]:
+                    feature_quant(b, g)
+            if 0 <= u - 1 < n_units:
+                b, h0 = UNITS[u - 1]
+                combine(u - 1)
+                interleave(u - 1)
+                for g in PASSES[h0]:
+                    transposes(b, g)
+            if u < n_units:
+                products(u)
+            for k in range(2):
+                if next_piece < len(pieces):
+                    piece_copy(next_piece)
+                    next_piece += 1
+            while quanted < next_piece - 1 or (next_piece == len(pieces) and quanted < next_piece):
+                piece_quant(quanted)
+                quanted += 1
+            if 0 <= u - 2:
+                b, h0 = UNITS[u - 2]
+                tail = u - 2 >= 6
+                if b == 1:
+                    for f in range(3 * h0 // 2, 3 * h0 // 2 + 3):
+                        dw_tile(f, tail)
+                if h0 == 6:
+                    for j in range(PACK):
+                        dx_tile(b, j, tail)

@@ -13,8 +13,6 @@ PACK = 4
 KP = P * PACK
 NPASS_J = J // KP
 NT = 512
-HU = 2
-WU = HU * D
 
 FLOPS = 2 * 2 * T * J * DIM
 BYTES = 2 * (T * DIM + 2 * S * 64 + J * DIM + T * H * DG) + 4 * (T * H * D + T * H + T * DIM + J * DIM)
@@ -28,7 +26,12 @@ E5 = mybir.dt.float8_e5m2_x4
 ADD = mybir.AluOpType.add
 MULT = mybir.AluOpType.mult
 
-UNITS = [(0, 0), (0, 2), (1, 0), (1, 2), (0, 4), (0, 6), (1, 4), (1, 6)]
+SLOTS = (0, 1, 2, 3)
+UNITS = [(0, 0, 2, SLOTS), (0, 2, 2, SLOTS), (1, 0, 2, SLOTS), (1, 2, 2, SLOTS), (0, 4, 2, SLOTS), (0, 6, 2, SLOTS), (1, 4, 2, SLOTS), (1, 6, 1, SLOTS), (1, 7, 1, (0,)), (1, 7, 1, (1,)), (1, 7, 1, (2,)), (1, 7, 1, (3,))]
+GCOMB = ()
+GPSUM = ()
+NBANK = 5
+NINT = {}
 
 
 def tile_lorentzmla_pb_v_kernel(tc, x, freqs_cos, freqs_sin, wq_w, wq_b, q_rot, t, grad_out, out_0, out_1):
@@ -37,6 +40,7 @@ def tile_lorentzmla_pb_v_kernel(tc, x, freqs_cos, freqs_sin, wq_w, wq_b, q_rot, 
         keep = ctx.enter_context(tc.tile_pool(name="keep", bufs=1))
         pool = ctx.enter_context(tc.tile_pool(name="work", bufs=2))
         psum = ctx.enter_context(tc.psum_pool(name="psum", bufs=1))
+        ctx.enter_context(tc.manual_schedule())
 
         t_sb = keep.tile([P, B, PACK, H], F32, name="t_sb")
         nc.sync.dma_start(out=t_sb[:], in_=t.rearrange("b (p j) h o -> p b j (h o)", j=PACK))
@@ -68,24 +72,26 @@ def tile_lorentzmla_pb_v_kernel(tc, x, freqs_cos, freqs_sin, wq_w, wq_b, q_rot, 
             raw_of[key] = raw
 
         load_g(0, 0, 2, 2)
-        load_q(0, 0, 2, 2, by_slot=True)
+        load_q(0, 0, 2, 3, by_slot=True)
         cs = keep.tile([P, 2, PACK * 64], BF16, name="cs")
         nc.sync.dma_start(out=cs[:, 0, :], in_=freqs_cos.rearrange("(p j) f -> p (j f)", j=PACK))
         nc.sync.dma_start(out=cs[:, 1, :], in_=freqs_sin.rearrange("(p j) f -> p (j f)", j=PACK))
-        load_raw(("x", 0), x[0])
         load_g(0, 2, 2, 2)
-        load_q(0, 2, 2, 2)
-        load_raw(("x", 1), x[1])
+        load_q(0, 2, 2, 3)
+        load_raw(("x", 0), x[0])
         load_g(1, 0, 4, 2)
-        load_q(1, 0, 4, 2)
-        load_raw(("w", 0), wq_w[0:KP, :])
+        load_q(1, 0, 2, 3)
+        load_raw(("x", 1), x[1])
+        load_q(1, 2, 2, 3)
         load_g(0, 4, 4, 2)
-        load_q(0, 4, 4, 2)
+        load_q(0, 4, 2, 3)
+        load_raw(("w", 0), wq_w[0:KP, :])
+        load_q(0, 6, 2, 3)
         load_raw(("w", 1), wq_w[KP:2 * KP, :])
-        load_raw(("w", 2), wq_w[2 * KP:3 * KP, :])
         load_g(1, 4, 4, 2)
-        load_q(1, 4, 4, 2)
-
+        load_q(1, 4, 2, 3)
+        load_raw(("w", 2), wq_w[2 * KP:3 * KP, :])
+        load_q(1, 6, 2, 3)
         ident = keep.tile([P, P], F32, name="ident")
         make_identity(nc, ident[:])
         ident_b = keep.tile([P, P], BF16, name="ident_b")
@@ -95,9 +101,11 @@ def tile_lorentzmla_pb_v_kernel(tc, x, freqs_cos, freqs_sin, wq_w, wq_b, q_rot, 
                                 scalar1=1.0, scalar2=0.0, op0=MULT, op1=ADD)
         nc.gpsimd.tensor_scalar(out=tab[:, 1, :, 0], in0=cs[:, 1, :], scalar1=-1.0, scalar2=0.0, op0=MULT, op1=ADD)
         nc.gpsimd.tensor_scalar(out=tab[:, 1, :, 1], in0=cs[:, 1, :], scalar1=1.0, scalar2=0.0, op0=MULT, op1=ADD)
-        tab_ps = psum.tile([P, 2, PACK * ROPE], BF16, name="tab_ps")
-        for k in range(2):
-            nc.tensor.matmul(tab_ps[:, k, :], lhsT=ident_b[:], rhs=tab[:, k, :, :].rearrange("p n e -> p (n e)"), start=True, stop=True)
+        tab_ps = psum.tile([P, 2, PACK * ROPE], BF16, name="tab")
+
+        def tables():
+            for k in range(2):
+                nc.tensor.matmul(tab_ps[:, k, :], lhsT=ident_b[:], rhs=tab[:, k, :, :].rearrange("p n e -> p (n e)"), start=True, stop=True)
 
         rt = keep.tile([P, B, PACK, H], F32, name="rt")
         nc.vector.reciprocal(out=rt[:], in_=t_sb[:])
@@ -116,84 +124,139 @@ def tile_lorentzmla_pb_v_kernel(tc, x, freqs_cos, freqs_sin, wq_w, wq_b, q_rot, 
         st = {}
 
         def coef(u):
-            b, h0 = UNITS[u]
+            b, h0, nh, js = UNITS[u]
+            j0, nj = js[0], len(js)
             g_t, go = g_of[(b, h0)]
-            c = pool.tile([P, PACK, HU], F32, name="c", bufs=3)
-            g0 = g_t[:, :, go:go + HU * DG].rearrange("p j (h d) -> p j h d", d=DG)[:, :, :, 0]
-            nc.vector.tensor_tensor(out=c[:], in0=g0, in1=rt[:, b, :, h0:h0 + HU], op=MULT)
+            c = pool.tile([P, PACK, 2], F32, name="c", bufs=3)
+            g0 = g_t[:, j0:j0 + nj, go:go + nh * DG].rearrange("p j (h d) -> p j h d", d=DG)[:, :, :, 0]
+            nc.vector.tensor_tensor(out=c[:, j0:j0 + nj, 0:nh], in0=g0, in1=rt[:, b, j0:j0 + nj, h0:h0 + nh], op=MULT)
             st[("c", u)] = c
 
+        def grads(u):
+            b, h0, nh, js = UNITS[u]
+            j0, nj = js[0], len(js)
+            g_t, go = g_of[(b, h0)]
+            st[("gp", u)] = []
+            for k in range(2):
+                gp = psum.tile([P, 2, nh * DG], BF16, name="gp", bufs=2)
+                for i in range(2):
+                    nc.tensor.matmul(gp[:, i, :], lhsT=ident_b[:], rhs=g_t[:, 2 * k + i, go:go + nh * DG], start=True, stop=True)
+                st[("gp", u)].append(gp)
+
         def lift(u):
-            b, h0 = UNITS[u]
+            b, h0, nh, js = UNITS[u]
+            j0, nj = js[0], len(js)
             c = st[("c", u)]
-            dr = pool.tile([P, PACK, HU, D], F32, name="dr", bufs=3)
+            dr = pool.tile([P, nj, nh, D], F32, name="dr", bufs=3)
             st[("dr", u)] = dr
-            for j in range(PACK):
-                for h in range(HU):
+            for j in js:
+                for h in range(nh):
                     q_t, qo = q_of[(b, h0 + h)]
                     g_t, go = g_of[(b, h0 + h)]
+                    if ("gp", u) in st:
+                        g = st[("gp", u)][j // 2][:, j % 2, h * DG + 1:(h + 1) * DG]
+                    else:
+                        g = g_t[:, j, go + 1:go + DG]
                     nc.vector.scalar_tensor_tensor(
-                        out=dr[:, j, h, :], in0=q_t[:, j, qo:qo + D], scalar=c[:, j, h:h + 1],
-                        in1=g_t[:, j, go + 1:go + DG], op0=MULT, op1=ADD)
-            nc.scalar.copy(out=da_of[b][:, :, h0 * D:(h0 + HU) * D].rearrange("p j (h d) -> p j h d", d=D)[:, :, :, 0:NOPE],
+                        out=dr[:, j - j0, h, :], in0=q_t[:, j, qo:qo + D], scalar=c[:, j, h:h + 1],
+                        in1=g, op0=MULT, op1=ADD)
+
+        def plain_part(u):
+            b, h0, nh, js = UNITS[u]
+            j0, nj = js[0], len(js)
+            dr = st[("dr", u)]
+            nc.scalar.copy(out=da_of[b][:, j0:j0 + nj, h0 * D:(h0 + nh) * D].rearrange("p j (h d) -> p j h d", d=D)[:, :, :, 0:NOPE],
                            in_=dr[:, :, :, 0:NOPE])
 
         def products(u):
+            b, h0, nh, js = UNITS[u]
+            j0, nj = js[0], len(js)
             dr = st[("dr", u)]
-            a = pool.tile([P, PACK, HU, ROPE], F32, name="a", bufs=2)
+            a = pool.tile([P, nj, nh, ROPE], F32, name="a", bufs=2)
             st[("a", u)] = a
 
             def table(k):
-                v = tab_ps[:, k, :].rearrange("p (j d) -> p j d", d=ROPE)
-                return v.unsqueeze(2).to_broadcast([P, PACK, HU, ROPE])
+                v = tab_ps[:, k, j0 * ROPE:(j0 + nj) * ROPE].rearrange("p (j d) -> p j d", d=ROPE)
+                return v.unsqueeze(2).to_broadcast([P, nj, nh, ROPE])
 
             pe = dr[:, :, :, NOPE:D]
             nc.vector.tensor_tensor(out=a[:], in0=pe, in1=table(0), op=MULT)
             nc.vector.tensor_tensor(out=pe, in0=pe, in1=table(1), op=MULT)
 
         def combine(u):
-            b, h0 = UNITS[u]
+            b, h0, nh, js = UNITS[u]
+            j0, nj = js[0], len(js)
             a, dr = st[("a", u)], st[("dr", u)]
-            dst = da_of[b][:, :, h0 * D:(h0 + HU) * D].rearrange("p j (h d) -> p j h d", d=D)[:, :, :, NOPE:D]
+            dst = da_of[b][:, j0:j0 + nj, h0 * D:(h0 + nh) * D].rearrange("p j (h d) -> p j h d", d=D)[:, :, :, NOPE:D]
             sw = dr[:, :, :, NOPE:D].rearrange("p j h (f e) -> p j h f e", e=2)[:, :, :, :, ::-1]
-            nc.vector.tensor_tensor(out=dst.rearrange("p j h (f e) -> p j h f e", e=2),
-                                    in0=a[:].rearrange("p j h (f e) -> p j h f e", e=2), in1=sw, op=ADD)
+            eng = nc.gpsimd if u in GCOMB else nc.vector
+            eng.tensor_tensor(out=dst.rearrange("p j h (f e) -> p j h f e", e=2),
+                              in0=a[:].rearrange("p j h (f e) -> p j h f e", e=2), in1=sw, op=ADD)
 
-        def interleave(u):
-            b, h0 = UNITS[u]
-            ti = pool.tile([P, WU, PACK], BF16, name="ti", bufs=3, align_bytes=64)
-            nc.gpsimd.tensor_scalar(out=ti[:], in0=da_of[b][:, :, h0 * D:(h0 + HU) * D].rearrange("p j w -> p w j"),
-                                    scalar1=1.0, scalar2=0.0, op0=MULT, op1=ADD)
-            st[("ti", u)] = ti
+        def interleave(b, h0, nh, parts=None):
+            ti = pool.tile([P, 2 * D, PACK], BF16, name="ti", bufs=3, align_bytes=64)
+            st[("ti", b, h0)] = ti
+            parts = parts or (("g", 0, nh * D),)
+            for (e, lo, hi) in parts:
+                src = da_of[b][:, :, h0 * D + lo:h0 * D + hi]
+                if e == "g":
+                    nc.gpsimd.tensor_scalar(out=ti[:, lo:hi, :], in0=src.rearrange("p j w -> p w j"), scalar1=1.0, scalar2=0.0, op0=MULT, op1=ADD)
+                else:
+                    f = nc.vector.tensor_copy if e == "v" else nc.scalar.copy
+                    f(out=ti[:, lo:hi, :].rearrange("p (c i) j -> p c j i", i=4), in_=src.rearrange("p j (c i) -> p c j i", i=4))
 
-        def token_quant(u):
-            b, h0 = UNITS[u]
-            ti = st[("ti", u)]
+        def token_quant(b, h0, nh):
+            ti = st[("ti", b, h0)]
             w0 = h0 * D
-            for (o, n) in ((0, 256), (256, 128)):
+            for (o, n) in (((0, 256), (256, 128)) if nh == 2 else ((0, 128), (128, 64))):
                 nc.vector.quantize_mx(out=tcd[:, b, w0 + o:w0 + o + n].bitcast(E5), scales=tsc[:, b, w0 + o:w0 + o + n],
                                       in_=ti[:, o:o + n, :].rearrange("p w j -> p (w j)"))
 
-        def transposes(b, g):
-            fi = pool.tile([P, S, PACK], BF16, name="fi", bufs=3, align_bytes=64)
-            st[("fi", b, g)] = fi
-            words = fi[:].rearrange("p n t -> p (n t)").bitcast(F32)
-            for jj in range(2):
-                tr = psum.tile([P, 2, 2, P], F32, name="tr", bufs=2)
-                for k in range(2):
-                    src = da_of[b][:, 2 * jj + k, :].bitcast(F32)
-                    for v in range(2):
-                        nc.tensor.transpose(tr[:, k, v, :], src[:, 256 * g + v:256 * (g + 1):2], ident[:])
-                nc.scalar.copy(out=words[:, 512 * jj:512 * (jj + 1)].rearrange("p (k r v) -> p k r v", k=2, v=2),
-                               in_=tr[:].rearrange("p k v r -> p k r v"))
+        def transposes(b, g, js):
+            if (b, g) not in st:
+                fi = pool.tile([P, S, PACK], BF16, name="fi", bufs=3, align_bytes=64)
+                st[(b, g)] = fi
+            tr = psum.tile([P, 2, 2, P], F32, name="tr", bufs=2)
+            for k, j in enumerate(js):
+                src = da_of[b][:, j, :].bitcast(F32)
+                for v in range(2):
+                    nc.tensor.transpose(tr[:, k, v, :], src[:, 256 * g + v:256 * (g + 1):2], ident[:])
+            st[("tr", b, g, js)] = tr
 
-        def feature_quant(b, g):
-            fi = st[("fi", b, g)]
-            nc.vector.quantize_mx(out=fcd[:, b, g, :].bitcast(E5), scales=fsc[:, b, g, :], in_=fi[:].rearrange("p n t -> p (n t)"))
+        def feature_copy(b, g, js, eng="s"):
+            words = st[(b, g)][:].rearrange("p n t -> p (n t)").bitcast(F32)
+            n = len(js)
+            f = nc.scalar.copy if eng == "s" else nc.vector.tensor_copy
+            f(out=words[:, 256 * js[0]:256 * (js[0] + n)].rearrange("p (k r v) -> p k r v", k=n, v=2),
+              in_=st[("tr", b, g, js)][:, 0:n, :, :].rearrange("p k v r -> p k r v"))
+
+        def feature_quant(b, g, js=SLOTS):
+            fi = st[(b, g)]
+            c = slice(js[0] * P, (js[0] + len(js)) * P)
+            nc.vector.quantize_mx(out=fcd[:, b, g, c].bitcast(E5), scales=fsc[:, b, g, c], in_=fi[:, c, :].rearrange("p n t -> p (n t)"))
 
         pieces = [("x", 0, 0), ("x", 0, 1), ("x", 1, 0), ("x", 1, 1)] + [("w", g, n) for g in range(3) for n in range(2)]
 
-        def piece_copy(i):
+        def piece_turn(i, bk):
+            kind, g, n = pieces[i]
+            raw = raw_of[(kind, g)]
+            s = pool.tile([P, NT, PACK], BF16, name="stage", bufs=3, align_bytes=64)
+            st[("piece", i)] = s
+            st[("pbank", i)] = []
+            for k in range(2):
+                pb = psum.tile([P, 2, NT], BF16, name="m%d" % bk[k])
+                for v in range(2):
+                    c0 = n * NT + (2 * k + v) * P
+                    nc.tensor.matmul(pb[:, v, :], lhsT=ident_b[:], rhs=raw[:, :, c0:c0 + P].rearrange("p t c -> p c t"), start=True, stop=True)
+                st[("pbank", i)].append(pb)
+
+        def piece_copy(i, engs="ss"):
+            s = st[("piece", i)]
+            for k in range(2):
+                f = nc.scalar.copy if engs[k] == "s" else nc.vector.tensor_copy
+                f(out=s[:, 256 * k:256 * (k + 1), :].rearrange("p c t -> p (c t)"), in_=st[("pbank", i)][k][:].rearrange("p v n -> p (v n)"))
+
+        def piece_direct(i):
             kind, g, n = pieces[i]
             raw = raw_of[(kind, g)]
             s = pool.tile([P, NT, PACK], BF16, name="stage", bufs=3, align_bytes=64)
@@ -208,72 +271,210 @@ def tile_lorentzmla_pb_v_kernel(tc, x, freqs_cos, freqs_sin, wq_w, wq_b, q_rot, 
             nc.vector.quantize_mx(out=codes[:, g, n * NT:(n + 1) * NT].bitcast(E4), scales=scales[:, g, n * NT:(n + 1) * NT],
                                   in_=s[:].rearrange("p n t -> p (n t)"))
 
-        evac_n = [0]
 
-        def evac(out, in_, tail):
-            if tail and evac_n[0] % 2 == 1:
-                nc.vector.tensor_copy(out=out, in_=in_)
-            else:
-                nc.scalar.copy(out=out, in_=in_)
-            evac_n[0] += 1
+        def new_bank(k):
+            return psum.tile([P, NT], F32, name="m%d" % k)
 
-        def dw_tile(f, tail=False):
-            o = pool.tile([P, DIM], F32, name="o", bufs=4)
-            for n in range(2):
-                acc = psum.tile([P, NT], F32, name="mm", bufs=5)
-                for b in range(B):
-                    nc.tensor.matmul_mx(out=acc[:], lhsT=tcd[:, b, f * P:(f + 1) * P].bitcast(E5), lhsT_scale=tsc[:, b, f * P:(f + 1) * P],
-                                        rhs=xc[:, b, n * NT:(n + 1) * NT].bitcast(E4), rhs_scale=xs[:, b, n * NT:(n + 1) * NT],
-                                        start=(b == 0), stop=(b == B - 1))
-                evac(o[:, n * NT:(n + 1) * NT], acc[:], tail)
-            nc.sync.dma_start(out=out_1[f * P:(f + 1) * P, :], in_=o[:])
+        def dw_group(f, n, bank):
+            acc = new_bank(bank)
+            for b in range(B):
+                nc.tensor.matmul_mx(out=acc[:], lhsT=tcd[:, b, f * P:(f + 1) * P].bitcast(E5), lhsT_scale=tsc[:, b, f * P:(f + 1) * P],
+                                    rhs=xc[:, b, n * NT:(n + 1) * NT].bitcast(E4), rhs_scale=xs[:, b, n * NT:(n + 1) * NT],
+                                    start=(b == 0), stop=(b == B - 1))
+            return acc
 
-        def dx_tile(b, j, tail=False):
-            o = pool.tile([P, DIM], F32, name="o", bufs=4)
-            for n in range(2):
-                acc = psum.tile([P, NT], F32, name="mm", bufs=5)
-                for g in range(NPASS_J):
-                    nc.tensor.matmul_mx(out=acc[:], lhsT=fcd[:, b, g, j * P:(j + 1) * P].bitcast(E5), lhsT_scale=fsc[:, b, g, j * P:(j + 1) * P],
-                                        rhs=wc[:, g, n * NT:(n + 1) * NT].bitcast(E4), rhs_scale=ws[:, g, n * NT:(n + 1) * NT],
-                                        start=(g == 0), stop=(g == NPASS_J - 1))
-                evac(o[:, n * NT:(n + 1) * NT], acc[:], tail)
-            nc.sync.dma_start(out=out_0[b].rearrange("(p j) d -> p j d", j=PACK)[:, j, :], in_=o[:])
+        def dx_group(b, j, n, acc, passes):
+            for g in passes:
+                nc.tensor.matmul_mx(out=acc[:], lhsT=fcd[:, b, g, j * P:(j + 1) * P].bitcast(E5), lhsT_scale=fsc[:, b, g, j * P:(j + 1) * P],
+                                    rhs=wc[:, g, n * NT:(n + 1) * NT].bitcast(E4), rhs_scale=ws[:, g, n * NT:(n + 1) * NT],
+                                    start=(g == 0), stop=(g == NPASS_J - 1))
 
-        PASSES = {0: [], 2: [0], 4: [1], 6: [2]}
+        outs = {}
+
+        def evac(key, n, acc, eng):
+            if key not in outs:
+                o = pool.tile([P, DIM], F32, name="o", bufs=4)
+                outs[key] = [o, 0]
+            o = outs[key][0]
+            (nc.scalar.copy if eng == "s" else nc.vector.tensor_copy)(out=o[:, n * NT:(n + 1) * NT], in_=acc[:])
+            outs[key][1] += 1
+            if outs[key][1] == 2:
+                kind, i, j = key
+                dst = out_1[i * P:(i + 1) * P, :] if kind == "dw" else out_0[i].rearrange("(p j) d -> p j d", j=PACK)[:, j, :]
+                nc.sync.dma_start(out=dst, in_=o[:])
+
         n_units = len(UNITS)
+        banks = [0]
+
+        def next_bank():
+            banks[0] += 1
+            return banks[0] % NBANK
+
+        def dw_tiles(f0, f1, engs="ss"):
+            for f in range(f0, f1):
+                for n in range(2):
+                    evac(("dw", f, 0), n, dw_group(f, n, next_bank()), engs[n])
+
+        def dx_tile(b, j, engs="ss"):
+            for n in range(2):
+                acc = new_bank(next_bank())
+                dx_group(b, j, n, acc, (0, 1, 2))
+                evac(("dx", b, j), n, acc, engs[n])
+
+        cp, qt = [0], [0]
+
+        def copies(k):
+            for i in range(k):
+                if cp[0] < len(pieces) - 1:
+                    piece_turn(cp[0], (next_bank(), next_bank()))
+                    piece_copy(cp[0])
+                else:
+                    piece_direct(cp[0])
+                cp[0] += 1
+
+        def piece_quants(k):
+            for i in range(k):
+                piece_quant(qt[0])
+                qt[0] += 1
+
+        tables()
         coef(0)
-        next_piece, quanted = 0, 0
-        for u in range(n_units + 2):
-            if u + 1 < n_units:
-                coef(u + 1)
-            if u < n_units:
-                lift(u)
-            if 0 <= u - 2:
-                b, h0 = UNITS[u - 2]
-                token_quant(u - 2)
-                for g in PASSES[h0]:
-                    feature_quant(b, g)
-            if 0 <= u - 1 < n_units:
-                b, h0 = UNITS[u - 1]
-                combine(u - 1)
-                interleave(u - 1)
-                for g in PASSES[h0]:
-                    transposes(b, g)
-            if u < n_units:
-                products(u)
-            for k in range(2):
-                if next_piece < len(pieces):
-                    piece_copy(next_piece)
-                    next_piece += 1
-            while quanted < next_piece - 1 or (next_piece == len(pieces) and quanted < next_piece):
-                piece_quant(quanted)
-                quanted += 1
-            if 0 <= u - 2:
-                b, h0 = UNITS[u - 2]
-                tail = u - 2 >= 6
-                if b == 1:
-                    for f in range(3 * h0 // 2, 3 * h0 // 2 + 3):
-                        dw_tile(f, tail)
-                if h0 == 6:
-                    for j in range(PACK):
-                        dx_tile(b, j, tail)
+        lift(0)
+        plain_part(0)
+        coef(1)
+        products(0)
+        lift(1)
+        combine(0)
+        interleave(0, 0, 2)
+        plain_part(1)
+        copies(2)
+        products(1)
+        coef(2)
+        token_quant(0, 0, 2)
+        lift(2)
+        combine(1)
+        interleave(0, 2, 2)
+        transposes(0, 0, (0, 1))
+        transposes(0, 0, (2, 3))
+        feature_copy(0, 0, (0, 1))
+        feature_copy(0, 0, (2, 3))
+        plain_part(2)
+        copies(2)
+        coef(3)
+        products(2)
+        piece_quants(2)
+        token_quant(0, 2, 2)
+        lift(3)
+        feature_quant(0, 0)
+        combine(2)
+        interleave(1, 0, 2)
+        plain_part(3)
+        copies(2)
+        coef(4)
+        products(3)
+        piece_quants(2)
+        token_quant(1, 0, 2)
+        dw_tiles(0, 3)
+        lift(4)
+        combine(3)
+        interleave(1, 2, 2)
+        transposes(1, 0, (0, 1))
+        transposes(1, 0, (2, 3))
+        feature_copy(1, 0, (0, 1))
+        feature_copy(1, 0, (2, 3))
+        plain_part(4)
+        copies(2)
+        coef(5)
+        products(4)
+        piece_quants(2)
+        token_quant(1, 2, 2)
+        dw_tiles(3, 5)
+        lift(5)
+        feature_quant(1, 0)
+        combine(4)
+        interleave(0, 4, 2)
+        transposes(0, 1, (0, 1))
+        transposes(0, 1, (2, 3))
+        feature_copy(0, 1, (0, 1))
+        feature_copy(0, 1, (2, 3))
+        plain_part(5)
+        dw_tiles(5, 6)
+        copies(2)
+        coef(6)
+        products(5)
+        piece_quants(1)
+        token_quant(0, 4, 2)
+        lift(6)
+        piece_quants(1)
+        feature_quant(0, 1)
+        combine(5)
+        interleave(0, 6, 2)
+        transposes(0, 2, (0, 1))
+        transposes(0, 2, (2, 3))
+        feature_copy(0, 2, (0, 1))
+        feature_copy(0, 2, (2, 3))
+        plain_part(6)
+        coef(7)
+        products(6)
+        piece_quants(2)
+        feature_quant(0, 2)
+        token_quant(0, 6, 2)
+        dx_tile(0, 0)
+        dx_tile(0, 1)
+        lift(7)
+        combine(6)
+        interleave(1, 4, 2)
+        transposes(1, 1, (0, 1))
+        transposes(1, 1, (2, 3))
+        feature_copy(1, 1, (0, 1))
+        feature_copy(1, 1, (2, 3))
+        plain_part(7)
+        dx_tile(0, 2)
+        dx_tile(0, 3)
+        coef(8)
+        coef(9)
+        products(7)
+        feature_quant(1, 1)
+        token_quant(1, 4, 2)
+        pre = {}
+        lift(8)
+        combine(7)
+        interleave(1, 6, 1)
+        plain_part(8)
+        products(8)
+        coef(10)
+        coef(11)
+        dw_tiles(6, 8)
+        banks[0] = 3
+        for k in range(3):
+            lift(9 + k)
+            combine(8 + k)
+            plain_part(9 + k)
+            transposes(1, 2, (k,))
+            feature_copy(1, 2, (k,))
+            products(9 + k)
+            if k == 0:
+                token_quant(1, 6, 1)
+                dw_tiles(8, 9)
+                for n in range(2):
+                    pre[(0, n)] = new_bank(next_bank())
+                    dx_group(1, 0, n, pre[(0, n)], (0, 1))
+            if k == 1:
+                feature_quant(1, 2, (0,))
+                dw_tiles(9, 10)
+                for n in range(2):
+                    dx_group(1, 0, n, pre[(0, n)], (2,))
+                    evac(("dx", 1, 0), n, pre[(0, n)], "s")
+            if k == 2:
+                feature_quant(1, 2, (1,))
+                dx_tile(1, 1)
+        combine(11)
+        interleave(1, 7, 1, (("v", 0, 128), ("s", 128, 192)))
+        transposes(1, 2, (3,))
+        feature_copy(1, 2, (3,), "v")
+        feature_quant(1, 2, (2,))
+        token_quant(1, 7, 1)
+        dx_tile(1, 2)
+        feature_quant(1, 2, (3,))
+        dw_tiles(10, 12, "sv")
+        dx_tile(1, 3, "sv")

@@ -27,11 +27,242 @@ ADD = mybir.AluOpType.add
 MULT = mybir.AluOpType.mult
 
 SLOTS = (0, 1, 2, 3)
-UNITS = [(0, 0, 2, SLOTS), (0, 2, 2, SLOTS), (1, 0, 2, SLOTS), (1, 2, 2, SLOTS), (0, 4, 2, SLOTS), (0, 6, 2, SLOTS), (1, 4, 2, SLOTS), (1, 6, 1, SLOTS), (1, 7, 1, (0,)), (1, 7, 1, (1,)), (1, 7, 1, (2,)), (1, 7, 1, (3,))]
-GCOMB = ()
-GPSUM = ()
-NBANK = 5
-NINT = {}
+UNITS = [(0, 0, 8, (0,)), (0, 0, 8, (1,)), (0, 0, 8, (2,)), (0, 0, 8, (3,)), (1, 0, 2, SLOTS), (1, 2, 2, SLOTS), (1, 4, 2, SLOTS), (1, 6, 1, SLOTS), (1, 7, 1, (0,)), (1, 7, 1, (1,)), (1, 7, 1, (2,)), (1, 7, 1, (3,))]
+NBANK = 6
+PLAN = [
+    ("coef", 0),
+    ("lift", 0),
+    ("prod", 0),
+    ("plain", 0),
+    ("coef", 1),
+    ("comb", 0),
+    ("lift", 1),
+    ("st", 0, 2, 1),
+    ("st", 0, 0, 2),
+    ("sc", 0, 2, 1, "s"),
+    ("pd", "w", 0, 1, 0, "s"),
+    ("pt", "w", 0, 0, 1),
+    ("pt", "w", 0, 0, 0),
+    ("coef", 2),
+    ("plain", 1),
+    ("prod", 1),
+    ("sc", 0, 0, 2, "s"),
+    ("pd", "w", 0, 1, 1, "s"),
+    ("lift", 2),
+    ("pc", "w", 0, 0, 0, "s"),
+    ("pc", "w", 0, 0, 1, "s"),
+    ("pt", "w", 1, 0, 1),
+    ("pd", "w", 1, 1, 1, "s"),
+    ("pq", "w", 0, 1),
+    ("pt", "w", 1, 0, 0),
+    ("plain", 2),
+    ("comb", 1),
+    ("pd", "w", 1, 1, 0, "s"),
+    ("pq", "w", 0, 0),
+    ("st", 1, 0, 2),
+    ("sq", 0),
+    ("st", 1, 2, 1),
+    ("pc", "w", 1, 0, 0, "s"),
+    ("pq", "w", 1, 1),
+    ("sc", 1, 0, 2, "s"),
+    ("prod", 2),
+    ("sc", 1, 2, 1, "s"),
+    ("pc", "w", 1, 0, 1, "s"),
+    ("pt", "w", 2, 0, 1),
+    ("pd", "w", 2, 1, 1, "s"),
+    ("pt", "w", 2, 0, 0),
+    ("pd", "w", 2, 1, 0, "s"),
+    ("sq", 1),
+    ("comb", 2),
+    ("pc", "w", 2, 0, 0, "s"),
+    ("pq", "w", 1, 0),
+    ("st", 2, 2, 1),
+    ("pc", "w", 2, 0, 1, "s"),
+    ("st", 2, 0, 2),
+    ("pq", "w", 2, 1),
+    ("sc", 2, 2, 1, "s"),
+    ("dx", 0, 0, 1, (0, 1, 2)),
+    ("sc", 2, 0, 2, "s"),
+    ("coef", 3),
+    ("coef", 5),
+    ("pq", "w", 2, 0),
+    ("dx", 0, 0, 0, (0, 1, 2)),
+    ("lift", 3),
+    ("dx", 0, 1, 1, (0, 1, 2)),
+    ("dxl", 0, 0, 0, "s"),
+    ("dx", 0, 1, 0, (0, 1, 2)),
+    ("dxl", 0, 0, 1, "v"),
+    ("plain", 3),
+    ("pt", "x", 0, 0, 1),
+    ("prod", 3),
+    ("pd", "x", 0, 1, 0, "s"),
+    ("pt", "x", 0, 0, 0),
+    ("dxl", 0, 1, 0, "s"),
+    ("dxl", 0, 1, 1, "s"),
+    ("lift", 5),
+    ("pd", "x", 0, 1, 1, "s"),
+    ("pc", "x", 0, 0, 0, "s"),
+    ("pq", "x", 0, 1),
+    ("plain", 5),
+    ("comb", 3),
+    ("pd", "x", 1, 0, 0, "s"),
+    ("coef", 6),
+    ("st", 3, 0, 2),
+    ("coef", 4),
+    ("sq", 2),
+    ("il", 0, 512, 1024, "s"),
+    ("lift", 6),
+    ("st", 3, 2, 1),
+    ("dx", 0, 2, 1, (0, 1, 2)),
+    ("dx", 0, 2, 0, (0, 1, 2)),
+    ("sc", 3, 2, 1, "v"),
+    ("plain", 6),
+    ("lift", 4),
+    ("dxl", 0, 2, 0, "s"),
+    ("sc", 3, 0, 2, "s"),
+    ("pd", "x", 1, 1, 1, "s"),
+    ("sq", 3),
+    ("dx", 0, 3, 0, (0, 1, 2)),
+    ("prod", 4),
+    ("plain", 4),
+    ("dx", 0, 3, 1, (0, 1, 2)),
+    ("pd", "x", 1, 0, 1, "s"),
+    ("dxl", 0, 3, 0, "s"),
+    ("tq", 0, 512, 1024),
+    ("dxl", 0, 3, 1, "s"),
+    ("comb", 4),
+    ("il", 0, 0, 512, "s"),
+    ("pq", "x", 1, 0),
+    ("prod", 5),
+    ("pd", "x", 1, 1, 0, "s"),
+    ("tq", 0, 0, 512),
+    ("pc", "x", 0, 0, 1, "s"),
+    ("pq", "x", 1, 1),
+    ("il", 1, 0, 384, "s"),
+    ("pq", "x", 0, 0),
+    ("comb", 5),
+    ("dxl", 0, 2, 1, "s"),
+    ("tq", 1, 0, 384),
+    ("tr", 0, (2, 3)),
+    ("il", 0, 1024, 1536, "s"),
+    ("prod", 6),
+    ("dw", 1, 0),
+    ("dw", 1, 1),
+    ("tr", 0, (0, 1)),
+    ("dw", 0, 0),
+    ("coef", 7),
+    ("il", 1, 384, 768, "v"),
+    ("fc", 0, (0, 1), "s"),
+    ("dw", 0, 1),
+    ("dwl", 1, 0, "s"),
+    ("comb", 6),
+    ("dw", 2, 1),
+    ("fc", 0, (2, 3), "s"),
+    ("dw", 2, 0),
+    ("dwl", 1, 1, "s"),
+    ("tq", 1, 384, 768),
+    ("tr", 1, (2, 3)),
+    ("dwl", 2, 0, "s"),
+    ("fq", 0, (0, 1, 2, 3)),
+    ("dwl", 2, 1, "s"),
+    ("tr", 1, (0, 1)),
+    ("tq", 0, 1024, 1536),
+    ("dw", 3, 1),
+    ("fc", 1, (2, 3), "s"),
+    ("fc", 1, (0, 1), "v"),
+    ("dwl", 0, 0, "s"),
+    ("dw", 3, 0),
+    ("il", 1, 768, 1152, "v"),
+    ("dwl", 0, 1, "s"),
+    ("dw", 4, 1),
+    ("dwl", 3, 0, "s"),
+    ("dw", 4, 0),
+    ("fq", 1, (0, 1, 2, 3)),
+    ("dwl", 3, 1, "s"),
+    ("dw", 5, 0),
+    ("tq", 1, 768, 1152),
+    ("dwl", 4, 0, "s"),
+    ("dw", 6, 0),
+    ("coef", 8),
+    ("lift", 7),
+    ("dwl", 4, 1, "s"),
+    ("dw", 5, 1),
+    ("dwl", 5, 0, "s"),
+    ("dw", 7, 0),
+    ("lift", 8, True),
+    ("plain", 7),
+    ("prod", 7),
+    ("dw", 7, 1),
+    ("dwl", 6, 0, "s"),
+    ("dw", 6, 1),
+    ("dwl", 5, 1, "s"),
+    ("prod", 8),
+    ("dw", 8, 0),
+    ("dwl", 7, 0, "s"),
+    ("comb", 7),
+    ("dw", 8, 1),
+    ("dwl", 6, 1, "s"),
+    ("comb", 8),
+    ("coef", 10),
+    ("il", 1, 1152, 1344, "v"),
+    ("tr", 2, (0,)),
+    ("dwl", 7, 1, "s"),
+    ("fc", 2, (0,), "v"),
+    ("dwl", 8, 0, "s"),
+    ("tq", 1, 1152, 1344),
+    ("dw", 9, 1),
+    ("fq", 2, (0,)),
+    ("dwl", 8, 1, "s"),
+    ("coef", 9),
+    ("coef", 11),
+    ("lift", 10, True),
+    ("dx", 1, 0, 1, (0, 1, 2)),
+    ("lift", 9, True),
+    ("prod", 10),
+    ("dx", 1, 0, 0, (0, 1, 2)),
+    ("prod", 9),
+    ("comb", 10),
+    ("lift", 11, True),
+    ("tr", 2, (2,)),
+    ("comb", 9),
+    ("dxl", 1, 0, 0, "s"),
+    ("dxl", 1, 0, 1, "v"),
+    ("tr", 2, (1,)),
+    ("dw", 9, 0),
+    ("fc", 2, (2,), "v"),
+    ("fc", 2, (1,), "s"),
+    ("prod", 11),
+    ("fq", 2, (2,)),
+    ("dx", 1, 2, 0, (0, 1, 2)),
+    ("dwl", 9, 0, "s"),
+    ("dwl", 9, 1, "v"),
+    ("comb", 11),
+    ("dx", 1, 2, 1, (0, 1, 2)),
+    ("fq", 2, (1,)),
+    ("dxl", 1, 2, 0, "v"),
+    ("dx", 1, 1, 1, (0, 1, 2)),
+    ("il", 1, 1344, 1536, "v"),
+    ("dxl", 1, 2, 1, "s"),
+    ("tq", 1, 1344, 1536),
+    ("dx", 1, 1, 0, (0, 1, 2)),
+    ("tr", 2, (3,)),
+    ("dxl", 1, 1, 0, "v"),
+    ("dxl", 1, 1, 1, "s"),
+    ("dw", 10, 0),
+    ("fc", 2, (3,), "v"),
+    ("dw", 10, 1),
+    ("fq", 2, (3,)),
+    ("dwl", 10, 0, "v"),
+    ("dx", 1, 3, 1, (0, 1, 2)),
+    ("dwl", 10, 1, "v"),
+    ("dx", 1, 3, 0, (0, 1, 2)),
+    ("dw", 11, 1),
+    ("dxl", 1, 3, 0, "s"),
+    ("dxl", 1, 3, 1, "v"),
+    ("dw", 11, 0),
+    ("dwl", 11, 0, "s"),
+    ("dwl", 11, 1, "v"),
+]
 
 
 def tile_lorentzmla_pb_v_kernel(tc, x, freqs_cos, freqs_sin, wq_w, wq_b, q_rot, t, grad_out, out_0, out_1):
@@ -46,12 +277,27 @@ def tile_lorentzmla_pb_v_kernel(tc, x, freqs_cos, freqs_sin, wq_w, wq_b, q_rot, 
         nc.sync.dma_start(out=t_sb[:], in_=t.rearrange("b (p j) h o -> p b j (h o)", j=PACK))
         q_of, g_of = {}, {}
 
+        def load_slot_g(j):
+            g_t = pool.tile([P, 1, H * DG], BF16, name="g2", bufs=2)
+            nc.sync.dma_start(out=g_t[:, 0, :], in_=grad_out[0].rearrange("(p j) h d -> p j (h d)", j=PACK)[:, j, :])
+            for h in range(H):
+                g_of[(0, h, j)] = (g_t, h * DG, j)
+
+        def load_slot_q(j, parts):
+            q_t = pool.tile([P, 1, H * D], F32, name="q2", bufs=4)
+            n = H * D // parts
+            for i in range(parts):
+                nc.sync.dma_start(out=q_t[:, 0, i * n:(i + 1) * n], in_=q_rot[0].rearrange("(p j) h d -> p j (h d)", j=PACK)[:, j, i * n:(i + 1) * n])
+            for h in range(H):
+                q_of[(0, h, j)] = (q_t, h * D, j)
+
         def load_g(b, h0, nh, bufs):
             g_t = pool.tile([P, PACK, nh * DG], BF16, name="g%d" % nh, bufs=bufs)
             src = grad_out[b].rearrange("(p j) h d -> p j (h d)", j=PACK)
             nc.sync.dma_start(out=g_t[:], in_=src[:, :, h0 * DG:(h0 + nh) * DG])
             for h in range(nh):
-                g_of[(b, h0 + h)] = (g_t, h * DG)
+                for j in range(PACK):
+                    g_of[(b, h0 + h, j)] = (g_t, h * DG, 0)
 
         def load_q(b, h0, nh, bufs, by_slot=False):
             q_t = pool.tile([P, PACK, nh * D], F32, name="q%d" % nh, bufs=bufs)
@@ -62,7 +308,8 @@ def tile_lorentzmla_pb_v_kernel(tc, x, freqs_cos, freqs_sin, wq_w, wq_b, q_rot, 
             else:
                 nc.sync.dma_start(out=q_t[:], in_=src)
             for h in range(nh):
-                q_of[(b, h0 + h)] = (q_t, h * D)
+                for j in range(PACK):
+                    q_of[(b, h0 + h, j)] = (q_t, h * D, 0)
 
         raw_of = {}
 
@@ -71,41 +318,35 @@ def tile_lorentzmla_pb_v_kernel(tc, x, freqs_cos, freqs_sin, wq_w, wq_b, q_rot, 
             nc.sync.dma_start(out=raw[:], in_=src.rearrange("(p j) d -> p j d", j=PACK))
             raw_of[key] = raw
 
-        load_g(0, 0, 2, 2)
-        load_q(0, 0, 2, 3, by_slot=True)
+        load_slot_g(0)
+        load_slot_q(0, 4)
         cs = keep.tile([P, 2, PACK * 64], BF16, name="cs")
         nc.sync.dma_start(out=cs[:, 0, :], in_=freqs_cos.rearrange("(p j) f -> p (j f)", j=PACK))
         nc.sync.dma_start(out=cs[:, 1, :], in_=freqs_sin.rearrange("(p j) f -> p (j f)", j=PACK))
-        load_g(0, 2, 2, 2)
-        load_q(0, 2, 2, 3)
-        load_raw(("x", 0), x[0])
-        load_g(1, 0, 4, 2)
-        load_q(1, 0, 2, 3)
-        load_raw(("x", 1), x[1])
-        load_q(1, 2, 2, 3)
-        load_g(0, 4, 4, 2)
-        load_q(0, 4, 2, 3)
+        load_slot_g(1)
+        load_slot_q(1, 1)
         load_raw(("w", 0), wq_w[0:KP, :])
-        load_q(0, 6, 2, 3)
+        load_slot_g(2)
+        load_slot_q(2, 1)
         load_raw(("w", 1), wq_w[KP:2 * KP, :])
-        load_g(1, 4, 4, 2)
-        load_q(1, 4, 2, 3)
+        load_slot_g(3)
+        load_slot_q(3, 1)
         load_raw(("w", 2), wq_w[2 * KP:3 * KP, :])
-        load_q(1, 6, 2, 3)
+        load_g(1, 0, 8, 1)
+        load_q(1, 0, 2, 4)
+        load_raw(("x", 0), x[0])
+        load_q(1, 2, 2, 4)
+        load_raw(("x", 1), x[1])
+        load_q(1, 4, 2, 4)
+        load_q(1, 6, 2, 4)
         ident = keep.tile([P, P], F32, name="ident")
         make_identity(nc, ident[:])
         ident_b = keep.tile([P, P], BF16, name="ident_b")
         make_identity(nc, ident_b[:])
         tab = keep.tile([P, 2, PACK * 64, 2], BF16, name="tab")
-        nc.gpsimd.tensor_scalar(out=tab[:, 0, :, :], in0=cs[:, 0, :].unsqueeze(2).to_broadcast([P, PACK * 64, 2]),
-                                scalar1=1.0, scalar2=0.0, op0=MULT, op1=ADD)
-        nc.gpsimd.tensor_scalar(out=tab[:, 1, :, 0], in0=cs[:, 1, :], scalar1=-1.0, scalar2=0.0, op0=MULT, op1=ADD)
-        nc.gpsimd.tensor_scalar(out=tab[:, 1, :, 1], in0=cs[:, 1, :], scalar1=1.0, scalar2=0.0, op0=MULT, op1=ADD)
-        tab_ps = psum.tile([P, 2, PACK * ROPE], BF16, name="tab")
-
-        def tables():
-            for k in range(2):
-                nc.tensor.matmul(tab_ps[:, k, :], lhsT=ident_b[:], rhs=tab[:, k, :, :].rearrange("p n e -> p (n e)"), start=True, stop=True)
+        nc.scalar.copy(out=tab[:, 0, :, :], in_=cs[:, 0, :].unsqueeze(2).to_broadcast([P, PACK * 64, 2]))
+        nc.scalar.activation(out=tab[:, 1, :, 0], in_=cs[:, 1, :], func=mybir.ActivationFunctionType.Copy, scale=-1.0)
+        nc.scalar.copy(out=tab[:, 1, :, 1], in_=cs[:, 1, :])
 
         rt = keep.tile([P, B, PACK, H], F32, name="rt")
         nc.vector.reciprocal(out=rt[:], in_=t_sb[:])
@@ -116,8 +357,10 @@ def tile_lorentzmla_pb_v_kernel(tc, x, freqs_cos, freqs_sin, wq_w, wq_b, q_rot, 
         ws = keep.tile([P, NPASS_J, DIM], U8, name="ws", align_bytes=64)
         tcd = keep.tile([P, B, J], U32, name="tcd", align_bytes=64)
         tsc = keep.tile([P, B, J], U8, name="tsc", align_bytes=64)
-        fcd = keep.tile([P, B, NPASS_J, S], U32, name="fcd", align_bytes=64)
-        fsc = keep.tile([P, B, NPASS_J, S], U8, name="fsc", align_bytes=64)
+        fc0 = keep.tile([P, S * NPASS_J], U32, name="fc0", align_bytes=64)
+        fs0 = keep.tile([P, S * NPASS_J], U8, name="fs0", align_bytes=64)
+        fcd = keep.tile([P, NPASS_J, S], U32, name="fcd", align_bytes=64)
+        fsc = keep.tile([P, NPASS_J, S], U8, name="fsc", align_bytes=64)
         da_of = [keep.tile([P, PACK, J], BF16, name="da0", align_bytes=64),
                  keep.tile([P, PACK, J], BF16, name="da1", align_bytes=64)]
 
@@ -126,24 +369,13 @@ def tile_lorentzmla_pb_v_kernel(tc, x, freqs_cos, freqs_sin, wq_w, wq_b, q_rot, 
         def coef(u):
             b, h0, nh, js = UNITS[u]
             j0, nj = js[0], len(js)
-            g_t, go = g_of[(b, h0)]
-            c = pool.tile([P, PACK, 2], F32, name="c", bufs=3)
-            g0 = g_t[:, j0:j0 + nj, go:go + nh * DG].rearrange("p j (h d) -> p j h d", d=DG)[:, :, :, 0]
-            nc.vector.tensor_tensor(out=c[:, j0:j0 + nj, 0:nh], in0=g0, in1=rt[:, b, j0:j0 + nj, h0:h0 + nh], op=MULT)
+            g_t, go, jb = g_of[(b, h0, j0)]
+            c = pool.tile([P, nj, nh], F32, name="c", bufs=3)
+            g0 = g_t[:, j0 - jb:j0 - jb + nj, go:go + nh * DG].rearrange("p j (h d) -> p j h d", d=DG)[:, :, :, 0]
+            nc.vector.tensor_tensor(out=c[:], in0=g0, in1=rt[:, b, j0:j0 + nj, h0:h0 + nh], op=MULT)
             st[("c", u)] = c
 
-        def grads(u):
-            b, h0, nh, js = UNITS[u]
-            j0, nj = js[0], len(js)
-            g_t, go = g_of[(b, h0)]
-            st[("gp", u)] = []
-            for k in range(2):
-                gp = psum.tile([P, 2, nh * DG], BF16, name="gp", bufs=2)
-                for i in range(2):
-                    nc.tensor.matmul(gp[:, i, :], lhsT=ident_b[:], rhs=g_t[:, 2 * k + i, go:go + nh * DG], start=True, stop=True)
-                st[("gp", u)].append(gp)
-
-        def lift(u):
+        def lift(u, direct=False):
             b, h0, nh, js = UNITS[u]
             j0, nj = js[0], len(js)
             c = st[("c", u)]
@@ -151,15 +383,14 @@ def tile_lorentzmla_pb_v_kernel(tc, x, freqs_cos, freqs_sin, wq_w, wq_b, q_rot, 
             st[("dr", u)] = dr
             for j in js:
                 for h in range(nh):
-                    q_t, qo = q_of[(b, h0 + h)]
-                    g_t, go = g_of[(b, h0 + h)]
-                    if ("gp", u) in st:
-                        g = st[("gp", u)][j // 2][:, j % 2, h * DG + 1:(h + 1) * DG]
-                    else:
-                        g = g_t[:, j, go + 1:go + DG]
-                    nc.vector.scalar_tensor_tensor(
-                        out=dr[:, j - j0, h, :], in0=q_t[:, j, qo:qo + D], scalar=c[:, j, h:h + 1],
-                        in1=g, op0=MULT, op1=ADD)
+                    q_t, qo, jb = q_of[(b, h0 + h, j)]
+                    g_t, go, jb = g_of[(b, h0 + h, j)]
+                    g = g_t[:, j - jb, go + 1:go + DG]
+                    parts = [(da_of[b][:, j, (h0 + h) * D:(h0 + h) * D + NOPE], 0, NOPE), (dr[:, j - j0, h, NOPE:D], NOPE, D)] if direct else [(dr[:, j - j0, h, :], 0, D)]
+                    for (o, lo, hi) in parts:
+                        nc.vector.scalar_tensor_tensor(
+                            out=o, in0=q_t[:, j - jb, qo + lo:qo + hi], scalar=c[:, j - j0, h:h + 1],
+                            in1=g[:, lo:hi], op0=MULT, op1=ADD)
 
         def plain_part(u):
             b, h0, nh, js = UNITS[u]
@@ -176,7 +407,7 @@ def tile_lorentzmla_pb_v_kernel(tc, x, freqs_cos, freqs_sin, wq_w, wq_b, q_rot, 
             st[("a", u)] = a
 
             def table(k):
-                v = tab_ps[:, k, j0 * ROPE:(j0 + nj) * ROPE].rearrange("p (j d) -> p j d", d=ROPE)
+                v = tab[:, k, :, :].rearrange("p (j f) e -> p j (f e)", j=PACK)[:, j0:j0 + nj, :]
                 return v.unsqueeze(2).to_broadcast([P, nj, nh, ROPE])
 
             pe = dr[:, :, :, NOPE:D]
@@ -189,292 +420,149 @@ def tile_lorentzmla_pb_v_kernel(tc, x, freqs_cos, freqs_sin, wq_w, wq_b, q_rot, 
             a, dr = st[("a", u)], st[("dr", u)]
             dst = da_of[b][:, j0:j0 + nj, h0 * D:(h0 + nh) * D].rearrange("p j (h d) -> p j h d", d=D)[:, :, :, NOPE:D]
             sw = dr[:, :, :, NOPE:D].rearrange("p j h (f e) -> p j h f e", e=2)[:, :, :, :, ::-1]
-            eng = nc.gpsimd if u in GCOMB else nc.vector
-            eng.tensor_tensor(out=dst.rearrange("p j h (f e) -> p j h f e", e=2),
+            nc.vector.tensor_tensor(out=dst.rearrange("p j h (f e) -> p j h f e", e=2),
                               in0=a[:].rearrange("p j h (f e) -> p j h f e", e=2), in1=sw, op=ADD)
 
-        def interleave(b, h0, nh, parts=None):
-            ti = pool.tile([P, 2 * D, PACK], BF16, name="ti", bufs=3, align_bytes=64)
-            st[("ti", b, h0)] = ti
-            parts = parts or (("g", 0, nh * D),)
-            for (e, lo, hi) in parts:
-                src = da_of[b][:, :, h0 * D + lo:h0 * D + hi]
-                if e == "g":
-                    nc.gpsimd.tensor_scalar(out=ti[:, lo:hi, :], in0=src.rearrange("p j w -> p w j"), scalar1=1.0, scalar2=0.0, op0=MULT, op1=ADD)
-                else:
-                    f = nc.vector.tensor_copy if e == "v" else nc.scalar.copy
-                    f(out=ti[:, lo:hi, :].rearrange("p (c i) j -> p c j i", i=4), in_=src.rearrange("p j (c i) -> p c j i", i=4))
+        def tile_of(key, shape, dt, name, bufs):
+            if key not in st:
+                st[key] = pool.tile(shape, dt, name=name, bufs=bufs, align_bytes=64)
+            return st[key]
 
-        def token_quant(b, h0, nh):
-            ti = st[("ti", b, h0)]
-            w0 = h0 * D
-            for (o, n) in (((0, 256), (256, 128)) if nh == 2 else ((0, 128), (128, 64))):
-                nc.vector.quantize_mx(out=tcd[:, b, w0 + o:w0 + o + n].bitcast(E5), scales=tsc[:, b, w0 + o:w0 + o + n],
-                                      in_=ti[:, o:o + n, :].rearrange("p w j -> p (w j)"))
+        def words_of(tile, pat):
+            return tile[:].rearrange(pat).bitcast(F32)
 
-        def transposes(b, g, js):
-            if (b, g) not in st:
-                fi = pool.tile([P, S, PACK], BF16, name="fi", bufs=3, align_bytes=64)
-                st[(b, g)] = fi
-            tr = psum.tile([P, 2, 2, P], F32, name="tr", bufs=2)
-            for k, j in enumerate(js):
-                src = da_of[b][:, j, :].bitcast(F32)
-                for v in range(2):
-                    nc.tensor.transpose(tr[:, k, v, :], src[:, 256 * g + v:256 * (g + 1):2], ident[:])
-            st[("tr", b, g, js)] = tr
-
-        def feature_copy(b, g, js, eng="s"):
-            words = st[(b, g)][:].rearrange("p n t -> p (n t)").bitcast(F32)
-            n = len(js)
-            f = nc.scalar.copy if eng == "s" else nc.vector.tensor_copy
-            f(out=words[:, 256 * js[0]:256 * (js[0] + n)].rearrange("p (k r v) -> p k r v", k=n, v=2),
-              in_=st[("tr", b, g, js)][:, 0:n, :, :].rearrange("p k v r -> p k r v"))
-
-        def feature_quant(b, g, js=SLOTS):
-            fi = st[(b, g)]
-            c = slice(js[0] * P, (js[0] + len(js)) * P)
-            nc.vector.quantize_mx(out=fcd[:, b, g, c].bitcast(E5), scales=fsc[:, b, g, c], in_=fi[:, c, :].rearrange("p n t -> p (n t)"))
-
-        pieces = [("x", 0, 0), ("x", 0, 1), ("x", 1, 0), ("x", 1, 1)] + [("w", g, n) for g in range(3) for n in range(2)]
-
-        def piece_turn(i, bk):
-            kind, g, n = pieces[i]
-            raw = raw_of[(kind, g)]
-            s = pool.tile([P, NT, PACK], BF16, name="stage", bufs=3, align_bytes=64)
-            st[("piece", i)] = s
-            st[("pbank", i)] = []
-            for k in range(2):
-                pb = psum.tile([P, 2, NT], BF16, name="m%d" % bk[k])
-                for v in range(2):
-                    c0 = n * NT + (2 * k + v) * P
-                    nc.tensor.matmul(pb[:, v, :], lhsT=ident_b[:], rhs=raw[:, :, c0:c0 + P].rearrange("p t c -> p c t"), start=True, stop=True)
-                st[("pbank", i)].append(pb)
-
-        def piece_copy(i, engs="ss"):
-            s = st[("piece", i)]
-            for k in range(2):
-                f = nc.scalar.copy if engs[k] == "s" else nc.vector.tensor_copy
-                f(out=s[:, 256 * k:256 * (k + 1), :].rearrange("p c t -> p (c t)"), in_=st[("pbank", i)][k][:].rearrange("p v n -> p (v n)"))
-
-        def piece_direct(i):
-            kind, g, n = pieces[i]
-            raw = raw_of[(kind, g)]
-            s = pool.tile([P, NT, PACK], BF16, name="stage", bufs=3, align_bytes=64)
-            st[("piece", i)] = s
-            nc.scalar.copy(out=s[:].rearrange("p (c i) t -> p c t i", i=4),
-                           in_=raw[:, :, n * NT:(n + 1) * NT].rearrange("p t (c i) -> p c t i", i=4))
-
-        def piece_quant(i):
-            kind, g, n = pieces[i]
-            s = st[("piece", i)]
-            codes, scales = (xc, xs) if kind == "x" else (wc, ws)
-            nc.vector.quantize_mx(out=codes[:, g, n * NT:(n + 1) * NT].bitcast(E4), scales=scales[:, g, n * NT:(n + 1) * NT],
-                                  in_=s[:].rearrange("p n t -> p (n t)"))
-
-
-        def new_bank(k):
-            return psum.tile([P, NT], F32, name="m%d" % k)
-
-        def dw_group(f, n, bank):
-            acc = new_bank(bank)
-            for b in range(B):
-                nc.tensor.matmul_mx(out=acc[:], lhsT=tcd[:, b, f * P:(f + 1) * P].bitcast(E5), lhsT_scale=tsc[:, b, f * P:(f + 1) * P],
-                                    rhs=xc[:, b, n * NT:(n + 1) * NT].bitcast(E4), rhs_scale=xs[:, b, n * NT:(n + 1) * NT],
-                                    start=(b == 0), stop=(b == B - 1))
-            return acc
-
-        def dx_group(b, j, n, acc, passes):
-            for g in passes:
-                nc.tensor.matmul_mx(out=acc[:], lhsT=fcd[:, b, g, j * P:(j + 1) * P].bitcast(E5), lhsT_scale=fsc[:, b, g, j * P:(j + 1) * P],
-                                    rhs=wc[:, g, n * NT:(n + 1) * NT].bitcast(E4), rhs_scale=ws[:, g, n * NT:(n + 1) * NT],
-                                    start=(g == 0), stop=(g == NPASS_J - 1))
-
-        outs = {}
-
-        def evac(key, n, acc, eng):
-            if key not in outs:
-                o = pool.tile([P, DIM], F32, name="o", bufs=4)
-                outs[key] = [o, 0]
-            o = outs[key][0]
-            (nc.scalar.copy if eng == "s" else nc.vector.tensor_copy)(out=o[:, n * NT:(n + 1) * NT], in_=acc[:])
-            outs[key][1] += 1
-            if outs[key][1] == 2:
-                kind, i, j = key
-                dst = out_1[i * P:(i + 1) * P, :] if kind == "dw" else out_0[i].rearrange("(p j) d -> p j d", j=PACK)[:, j, :]
-                nc.sync.dma_start(out=dst, in_=o[:])
-
-        n_units = len(UNITS)
+        copier = {"s": nc.scalar.copy, "v": nc.vector.tensor_copy}
         banks = [0]
 
-        def next_bank():
+        def new_bank(shape, dt):
             banks[0] += 1
-            return banks[0] % NBANK
+            return psum.tile(shape, dt, name="m%d" % (banks[0] % NBANK))
 
-        def dw_tiles(f0, f1, engs="ss"):
-            for f in range(f0, f1):
-                for n in range(2):
-                    evac(("dw", f, 0), n, dw_group(f, n, next_bank()), engs[n])
+        def turn(eng, out, src):
+            if eng == "g":
+                nc.gpsimd.tensor_scalar(out=out, in0=src.rearrange("p j w -> p w j"), scalar1=1.0, scalar2=0.0, op0=MULT, op1=ADD)
+            else:
+                copier[eng](out=out.rearrange("p (c i) j -> p c j i", i=4), in_=src.rearrange("p j (c i) -> p c j i", i=4))
 
-        def dx_tile(b, j, engs="ss"):
-            for n in range(2):
-                acc = new_bank(next_bank())
-                dx_group(b, j, n, acc, (0, 1, 2))
-                evac(("dx", b, j), n, acc, engs[n])
+        def interleave(b, w0, w1, eng):
+            ti = tile_of(("ti", b, w0), [P, NT, PACK], BF16, "ti", 3)
+            turn(eng, ti[:, 0:w1 - w0, :], da_of[b][:, :, w0:w1])
 
-        cp, qt = [0], [0]
+        def token_quant(b, w0, w1):
+            ti = st[("ti", b, w0)]
+            o = 0
+            while o < w1 - w0:
+                n = [k for k in (512, 256, 128, 64) if k <= w1 - w0 - o][0]
+                c = slice(w0 + o, w0 + o + n)
+                nc.vector.quantize_mx(out=tcd[:, b, c].bitcast(E5), scales=tsc[:, b, c], in_=ti[:, o:o + n, :].rearrange("p w j -> p (w j)"))
+                o += n
 
-        def copies(k):
-            for i in range(k):
-                if cp[0] < len(pieces) - 1:
-                    piece_turn(cp[0], (next_bank(), next_bank()))
-                    piece_copy(cp[0])
-                else:
-                    piece_direct(cp[0])
-                cp[0] += 1
+        def slot_turn(j, g0, ng):
+            src = da_of[0][:, j, :].bitcast(F32)
+            tr = psum.tile([P, 2, 2, P], F32, name="tr", bufs=2)
+            for k in range(ng):
+                for v in range(2):
+                    nc.tensor.transpose(tr[:, k, v, :], src[:, 256 * (g0 + k) + v:256 * (g0 + k + 1):2], ident[:])
+            st[("str", j, g0)] = tr
 
-        def piece_quants(k):
-            for i in range(k):
-                piece_quant(qt[0])
-                qt[0] += 1
+        def slot_copy(j, g0, ng, eng):
+            fs = tile_of(("fs", j), [P, NPASS_J, P, PACK], BF16, "fs", 2)
+            words = words_of(fs, "p g r t -> p (g r t)")
+            copier[eng](out=words[:, 256 * g0:256 * (g0 + ng)].rearrange("p (k r v) -> p k r v", k=ng, v=2),
+                        in_=st[("str", j, g0)][:, 0:ng, :, :].rearrange("p k v r -> p k r v"))
 
-        tables()
-        coef(0)
-        lift(0)
-        plain_part(0)
-        coef(1)
-        products(0)
-        lift(1)
-        combine(0)
-        interleave(0, 0, 2)
-        plain_part(1)
-        copies(2)
-        products(1)
-        coef(2)
-        token_quant(0, 0, 2)
-        lift(2)
-        combine(1)
-        interleave(0, 2, 2)
-        transposes(0, 0, (0, 1))
-        transposes(0, 0, (2, 3))
-        feature_copy(0, 0, (0, 1))
-        feature_copy(0, 0, (2, 3))
-        plain_part(2)
-        copies(2)
-        coef(3)
-        products(2)
-        piece_quants(2)
-        token_quant(0, 2, 2)
-        lift(3)
-        feature_quant(0, 0)
-        combine(2)
-        interleave(1, 0, 2)
-        plain_part(3)
-        copies(2)
-        coef(4)
-        products(3)
-        piece_quants(2)
-        token_quant(1, 0, 2)
-        dw_tiles(0, 3)
-        lift(4)
-        combine(3)
-        interleave(1, 2, 2)
-        transposes(1, 0, (0, 1))
-        transposes(1, 0, (2, 3))
-        feature_copy(1, 0, (0, 1))
-        feature_copy(1, 0, (2, 3))
-        plain_part(4)
-        copies(2)
-        coef(5)
-        products(4)
-        piece_quants(2)
-        token_quant(1, 2, 2)
-        dw_tiles(3, 5)
-        lift(5)
-        feature_quant(1, 0)
-        combine(4)
-        interleave(0, 4, 2)
-        transposes(0, 1, (0, 1))
-        transposes(0, 1, (2, 3))
-        feature_copy(0, 1, (0, 1))
-        feature_copy(0, 1, (2, 3))
-        plain_part(5)
-        dw_tiles(5, 6)
-        copies(2)
-        coef(6)
-        products(5)
-        piece_quants(1)
-        token_quant(0, 4, 2)
-        lift(6)
-        piece_quants(1)
-        feature_quant(0, 1)
-        combine(5)
-        interleave(0, 6, 2)
-        transposes(0, 2, (0, 1))
-        transposes(0, 2, (2, 3))
-        feature_copy(0, 2, (0, 1))
-        feature_copy(0, 2, (2, 3))
-        plain_part(6)
-        coef(7)
-        products(6)
-        piece_quants(2)
-        feature_quant(0, 2)
-        token_quant(0, 6, 2)
-        dx_tile(0, 0)
-        dx_tile(0, 1)
-        lift(7)
-        combine(6)
-        interleave(1, 4, 2)
-        transposes(1, 1, (0, 1))
-        transposes(1, 1, (2, 3))
-        feature_copy(1, 1, (0, 1))
-        feature_copy(1, 1, (2, 3))
-        plain_part(7)
-        dx_tile(0, 2)
-        dx_tile(0, 3)
-        coef(8)
-        coef(9)
-        products(7)
-        feature_quant(1, 1)
-        token_quant(1, 4, 2)
-        pre = {}
-        lift(8)
-        combine(7)
-        interleave(1, 6, 1)
-        plain_part(8)
-        products(8)
-        coef(10)
-        coef(11)
-        dw_tiles(6, 8)
-        banks[0] = 3
-        for k in range(3):
-            lift(9 + k)
-            combine(8 + k)
-            plain_part(9 + k)
-            transposes(1, 2, (k,))
-            feature_copy(1, 2, (k,))
-            products(9 + k)
-            if k == 0:
-                token_quant(1, 6, 1)
-                dw_tiles(8, 9)
-                for n in range(2):
-                    pre[(0, n)] = new_bank(next_bank())
-                    dx_group(1, 0, n, pre[(0, n)], (0, 1))
-            if k == 1:
-                feature_quant(1, 2, (0,))
-                dw_tiles(9, 10)
-                for n in range(2):
-                    dx_group(1, 0, n, pre[(0, n)], (2,))
-                    evac(("dx", 1, 0), n, pre[(0, n)], "s")
-            if k == 2:
-                feature_quant(1, 2, (1,))
-                dx_tile(1, 1)
-        combine(11)
-        interleave(1, 7, 1, (("v", 0, 128), ("s", 128, 192)))
-        transposes(1, 2, (3,))
-        feature_copy(1, 2, (3,), "v")
-        feature_quant(1, 2, (2,))
-        token_quant(1, 7, 1)
-        dx_tile(1, 2)
-        feature_quant(1, 2, (3,))
-        dw_tiles(10, 12, "sv")
-        dx_tile(1, 3, "sv")
+        def slot_quant(j):
+            fi = st[("fs", j)][:].rearrange("p g r t -> p (g r t)")
+            for (lo, n) in ((0, 256), (256, 128)):
+                c = slice(j * NPASS_J * P + lo, j * NPASS_J * P + lo + n)
+                nc.vector.quantize_mx(out=fc0[:, c].bitcast(E5), scales=fs0[:, c], in_=fi[:, 4 * lo:4 * (lo + n)])
+
+        def feature_turn(g, js):
+            tr = psum.tile([P, 2, 2, P], F32, name="tr", bufs=2)
+            for k, j in enumerate(js):
+                src = da_of[1][:, j, :].bitcast(F32)
+                for v in range(2):
+                    nc.tensor.transpose(tr[:, k, v, :], src[:, 256 * g + v:256 * (g + 1):2], ident[:])
+            st[("tr", g, js)] = tr
+
+        def feature_copy(g, js, eng):
+            fi = tile_of(("fi", g), [P, S, PACK], BF16, "fi", 3)
+            n = len(js)
+            copier[eng](out=words_of(fi, "p n t -> p (n t)")[:, 256 * js[0]:256 * (js[0] + n)].rearrange("p (k r v) -> p k r v", k=n, v=2),
+                        in_=st[("tr", g, js)][:, 0:n, :, :].rearrange("p k v r -> p k r v"))
+
+        def feature_quant(g, js):
+            c = slice(js[0] * P, (js[0] + len(js)) * P)
+            nc.vector.quantize_mx(out=fcd[:, g, c].bitcast(E5), scales=fsc[:, g, c], in_=st[("fi", g)][:, c, :].rearrange("p n t -> p (n t)"))
+
+        def piece_turn(kind, g, n, k):
+            raw = raw_of[(kind, g)]
+            pb = new_bank([P, 2, NT], BF16)
+            st[("pb", kind, g, n, k)] = pb
+            for v in range(2):
+                c0 = n * NT + (2 * k + v) * P
+                nc.tensor.matmul(pb[:, v, :], lhsT=ident_b[:], rhs=raw[:, :, c0:c0 + P].rearrange("p t c -> p c t"), start=True, stop=True)
+
+        def piece_copy(kind, g, n, k, eng):
+            s = tile_of(("stage", kind, g, n), [P, NT, PACK], BF16, "stage", 3)
+            copier[eng](out=s[:, 256 * k:256 * (k + 1), :].rearrange("p c t -> p (c t)"),
+                        in_=st[("pb", kind, g, n, k)][:].rearrange("p v n -> p (v n)"))
+
+        def piece_direct(kind, g, n, k, eng):
+            s = tile_of(("stage", kind, g, n), [P, NT, PACK], BF16, "stage", 3)
+            turn(eng, s[:, 256 * k:256 * (k + 1), :], raw_of[(kind, g)][:, :, n * NT + 256 * k:n * NT + 256 * (k + 1)])
+
+        def piece_quant(kind, g, n):
+            codes, scales = (xc, xs) if kind == "x" else (wc, ws)
+            c = slice(n * NT, (n + 1) * NT)
+            nc.vector.quantize_mx(out=codes[:, g, c].bitcast(E4), scales=scales[:, g, c], in_=st[("stage", kind, g, n)][:].rearrange("p n t -> p (n t)"))
+
+        def dw_multiply(f, n):
+            acc = new_bank([P, NT], F32)
+            st[("dw", f, n)] = acc
+            r, c = slice(f * P, (f + 1) * P), slice(n * NT, (n + 1) * NT)
+            for b in range(B):
+                nc.tensor.matmul_mx(out=acc[:], lhsT=tcd[:, b, r].bitcast(E5), lhsT_scale=tsc[:, b, r],
+                                    rhs=xc[:, b, c].bitcast(E4), rhs_scale=xs[:, b, c], start=(b == 0), stop=(b == B - 1))
+
+        def dx_codes(b, j, g):
+            if b == 0:
+                c = slice((j * NPASS_J + g) * P, (j * NPASS_J + g + 1) * P)
+                return fc0[:, c], fs0[:, c]
+            return fcd[:, g, j * P:(j + 1) * P], fsc[:, g, j * P:(j + 1) * P]
+
+        def dx_multiply(b, j, n, passes):
+            if passes[0] == 0:
+                st[("dx", b, j, n)] = new_bank([P, NT], F32)
+            c = slice(n * NT, (n + 1) * NT)
+            for g in passes:
+                codes, scales = dx_codes(b, j, g)
+                nc.tensor.matmul_mx(out=st[("dx", b, j, n)][:], lhsT=codes.bitcast(E5), lhsT_scale=scales,
+                                    rhs=wc[:, g, c].bitcast(E4), rhs_scale=ws[:, g, c], start=(g == 0), stop=(g == NPASS_J - 1))
+
+        def leave(key, n, eng, dst):
+            o = tile_of(("o",) + key, [P, DIM], F32, "o", 4)
+            copier[eng](out=o[:, n * NT:(n + 1) * NT], in_=st[key + (n,)][:])
+            left[key] = left.get(key, 0) + 1
+            if left[key] == 2:
+                nc.sync.dma_start(out=dst, in_=o[:])
+
+        left = {}
+
+        def dw_leave(f, n, eng):
+            leave(("dw", f), n, eng, out_1[f * P:(f + 1) * P, :])
+
+        def dx_leave(b, j, n, eng):
+            leave(("dx", b, j), n, eng, out_0[b].rearrange("(p j) d -> p j d", j=PACK)[:, j, :])
+
+        steps = {"coef": coef, "lift": lift, "plain": plain_part, "prod": products, "comb": combine,
+                 "il": interleave, "tq": token_quant, "st": slot_turn, "sc": slot_copy, "sq": slot_quant,
+                 "tr": feature_turn, "fc": feature_copy, "fq": feature_quant,
+                 "pt": piece_turn, "pc": piece_copy, "pd": piece_direct, "pq": piece_quant,
+                 "dw": dw_multiply, "dwl": dw_leave, "dx": dx_multiply, "dxl": dx_leave}
+
+        def run_step(step):
+            steps[step[0]](*step[1:])
+
+        for step in PLAN:
+            run_step(step)

@@ -27,241 +27,236 @@ ADD = mybir.AluOpType.add
 MULT = mybir.AluOpType.mult
 
 SLOTS = (0, 1, 2, 3)
-UNITS = [(0, 0, 8, (0,)), (0, 0, 8, (1,)), (0, 0, 8, (2,)), (0, 0, 8, (3,)), (1, 0, 2, SLOTS), (1, 2, 2, SLOTS), (1, 4, 2, SLOTS), (1, 6, 1, SLOTS), (1, 7, 1, (0,)), (1, 7, 1, (1,)), (1, 7, 1, (2,)), (1, 7, 1, (3,))]
-NBANK = 6
+UNITS = [(0, 0, 8, (0,)), (0, 0, 8, (1,)), (0, 0, 8, (2,)), (0, 0, 8, (3,)), (1, 0, 2, SLOTS), (1, 2, 2, SLOTS), (1, 4, 2, SLOTS), (1, 6, 1, SLOTS), (1, 7, 1, (0, 1)), (1, 7, 1, (2, 3))]
+NBANK = 5
 PLAN = [
-    ("coef", 0),
+    ("coef", 0, 0, 1),
     ("lift", 0),
+    ("pt", "w", 0, 1, 0, "m2"),
+    ("pc", "w", 0, 1, 0, "s"),
     ("prod", 0),
-    ("plain", 0),
-    ("coef", 1),
-    ("comb", 0),
+    ("coef", 0, 1, 1),
     ("lift", 1),
-    ("st", 0, 2, 1),
+    ("plain", 1, "s"),
+    ("pt", "w", 0, 0, 0, "m2"),
+    ("plain", 0, "s"),
+    ("comb", 0),
     ("st", 0, 0, 2),
-    ("sc", 0, 2, 1, "s"),
-    ("pd", "w", 0, 1, 0, "s"),
-    ("pt", "w", 0, 0, 1),
-    ("pt", "w", 0, 0, 0),
-    ("coef", 2),
-    ("plain", 1),
-    ("prod", 1),
-    ("sc", 0, 0, 2, "s"),
-    ("pd", "w", 0, 1, 1, "s"),
-    ("lift", 2),
+    ("coef", 0, 2, 1),
     ("pc", "w", 0, 0, 0, "s"),
-    ("pc", "w", 0, 0, 1, "s"),
-    ("pt", "w", 1, 0, 1),
-    ("pd", "w", 1, 1, 1, "s"),
-    ("pq", "w", 0, 1),
-    ("pt", "w", 1, 0, 0),
-    ("plain", 2),
+    ("prod", 1),
+    ("pt", "w", 1, 1, 0, "m5"),
+    ("st", 0, 2, 1),
+    ("sc", 0, 0, 2, "s"),
+    ("lift", 2),
     ("comb", 1),
-    ("pd", "w", 1, 1, 0, "s"),
-    ("pq", "w", 0, 0),
-    ("st", 1, 0, 2),
-    ("sq", 0),
-    ("st", 1, 2, 1),
-    ("pc", "w", 1, 0, 0, "s"),
-    ("pq", "w", 1, 1),
-    ("sc", 1, 0, 2, "s"),
+    ("pt", "w", 0, 1, 1, "m1"),
+    ("coef", 0, 3, 1),
+    ("pc", "w", 0, 1, 1, "s"),
+    ("plain", 2, "s"),
     ("prod", 2),
-    ("sc", 1, 2, 1, "s"),
-    ("pc", "w", 1, 0, 1, "s"),
-    ("pt", "w", 2, 0, 1),
-    ("pd", "w", 2, 1, 1, "s"),
-    ("pt", "w", 2, 0, 0),
-    ("pd", "w", 2, 1, 0, "s"),
-    ("sq", 1),
+    ("pt", "w", 1, 1, 1, "m4"),
+    ("pc", "w", 1, 1, 1, "s"),
+    ("st", 1, 2, 1),
+    ("pt", "w", 0, 0, 1, "m2"),
+    ("pt", "w", 1, 0, 0, "m3"),
+    ("pc", "w", 1, 1, 0, "s"),
+    ("pt", "w", 2, 0, 1, "m5"),
+    ("pt", "w", 2, 1, 0, "m4"),
+    ("pq", "w", 0, 1),
     ("comb", 2),
+    ("sc", 1, 2, 1, "s"),
+    ("pc", "w", 0, 0, 1, "s"),
+    ("pq", "w", 0, 0),
+    ("pt", "w", 2, 0, 0, "m1"),
+    ("pc", "w", 1, 0, 0, "s"),
+    ("sc", 0, 2, 1, "s"),
+    ("sq", 0),
+    ("pt", "w", 1, 0, 1, "m3"),
+    ("st", 2, 2, 1),
+    ("sc", 2, 2, 1, "s"),
+    ("lift", 3),
+    ("st", 1, 0, 2),
+    ("sc", 1, 0, 2, "s"),
+    ("pq", "w", 1, 1),
+    ("pc", "w", 1, 0, 1, "s"),
+    ("coef", 1, 0, 4),
+    ("st", 2, 0, 2),
+    ("pt", "w", 2, 1, 1, "m0"),
+    ("prod", 3),
+    ("pc", "w", 2, 1, 0, "s"),
+    ("sc", 2, 0, 2, "s"),
+    ("pc", "w", 2, 0, 1, "s"),
+    ("pc", "w", 2, 1, 1, "s"),
     ("pc", "w", 2, 0, 0, "s"),
     ("pq", "w", 1, 0),
-    ("st", 2, 2, 1),
-    ("pc", "w", 2, 0, 1, "s"),
-    ("st", 2, 0, 2),
-    ("pq", "w", 2, 1),
-    ("sc", 2, 2, 1, "s"),
-    ("dx", 0, 0, 1, (0, 1, 2)),
-    ("sc", 2, 0, 2, "s"),
-    ("coef", 3),
-    ("coef", 5),
+    ("plain", 3, "s"),
     ("pq", "w", 2, 0),
-    ("dx", 0, 0, 0, (0, 1, 2)),
-    ("lift", 3),
-    ("dx", 0, 1, 1, (0, 1, 2)),
-    ("dxl", 0, 0, 0, "s"),
-    ("dx", 0, 1, 0, (0, 1, 2)),
-    ("dxl", 0, 0, 1, "v"),
-    ("plain", 3),
-    ("pt", "x", 0, 0, 1),
-    ("prod", 3),
-    ("pd", "x", 0, 1, 0, "s"),
-    ("pt", "x", 0, 0, 0),
-    ("dxl", 0, 1, 0, "s"),
-    ("dxl", 0, 1, 1, "s"),
-    ("lift", 5),
+    ("dx", 0, 0, 0, (0, 1, 2), "m5"),
     ("pd", "x", 0, 1, 1, "s"),
+    ("pt", "x", 0, 0, 1, "m1"),
+    ("dxl", 0, 0, 0, "s"),
+    ("comb", 3),
+    ("il", 0, 0, 512, "s"),
+    ("pt", "x", 1, 0, 0, "m5"),
+    ("sq", 1),
+    ("dx", 0, 1, 0, (0, 1, 2), "m2"),
+    ("pd", "x", 0, 1, 0, "s"),
+    ("dxl", 0, 1, 0, "s"),
+    ("lift", 4),
+    ("plain", 4, "s"),
+    ("lift", 5),
+    ("plain", 5, "s"),
+    ("pq", "w", 2, 1),
+    ("dx", 0, 0, 1, (0, 1, 2), "m4"),
+    ("dxl", 0, 0, 1, "s"),
+    ("prod", 4),
+    ("prod", 5),
+    ("dx", 0, 1, 1, (0, 1, 2), "m3"),
+    ("dxl", 0, 1, 1, "s"),
+    ("pc", "x", 0, 0, 1, "s"),
+    ("sq", 2),
+    ("comb", 4),
+    ("tq", 0, 0, 512),
+    ("pt", "x", 1, 0, 1, "m4"),
+    ("pc", "x", 1, 0, 1, "s"),
+    ("comb", 5),
+    ("st", 3, 0, 2),
+    ("st", 3, 2, 1),
+    ("sc", 3, 0, 2, "s"),
+    ("sc", 3, 2, 1, "s"),
+    ("il", 0, 512, 1024, "s"),
+    ("sq", 3),
+    ("pt", "x", 0, 0, 0, "m1"),
+    ("il", 1, 0, 384, "v"),
+    ("dx", 0, 2, 0, (0, 1, 2), "m0"),
+    ("dxl", 0, 2, 0, "s"),
+    ("dx", 0, 2, 1, (0, 1, 2), "m0"),
     ("pc", "x", 0, 0, 0, "s"),
     ("pq", "x", 0, 1),
-    ("plain", 5),
-    ("comb", 3),
-    ("pd", "x", 1, 0, 0, "s"),
-    ("coef", 6),
-    ("st", 3, 0, 2),
-    ("coef", 4),
-    ("sq", 2),
-    ("il", 0, 512, 1024, "s"),
-    ("lift", 6),
-    ("st", 3, 2, 1),
-    ("dx", 0, 2, 1, (0, 1, 2)),
-    ("dx", 0, 2, 0, (0, 1, 2)),
-    ("sc", 3, 2, 1, "v"),
-    ("plain", 6),
-    ("lift", 4),
-    ("dxl", 0, 2, 0, "s"),
-    ("sc", 3, 0, 2, "s"),
-    ("pd", "x", 1, 1, 1, "s"),
-    ("sq", 3),
-    ("dx", 0, 3, 0, (0, 1, 2)),
-    ("prod", 4),
-    ("plain", 4),
-    ("dx", 0, 3, 1, (0, 1, 2)),
-    ("pd", "x", 1, 0, 1, "s"),
-    ("dxl", 0, 3, 0, "s"),
+    ("dx", 0, 3, 1, (0, 1, 2), "m4"),
+    ("dx", 0, 3, 0, (0, 1, 2), "m5"),
+    ("pc", "x", 1, 0, 0, "s"),
     ("tq", 0, 512, 1024),
-    ("dxl", 0, 3, 1, "s"),
-    ("comb", 4),
-    ("il", 0, 0, 512, "s"),
     ("pq", "x", 1, 0),
-    ("prod", 5),
-    ("pd", "x", 1, 1, 0, "s"),
-    ("tq", 0, 0, 512),
-    ("pc", "x", 0, 0, 1, "s"),
-    ("pq", "x", 1, 1),
-    ("il", 1, 0, 384, "s"),
-    ("pq", "x", 0, 0),
-    ("comb", 5),
-    ("dxl", 0, 2, 1, "s"),
-    ("tq", 1, 0, 384),
     ("tr", 0, (2, 3)),
+    ("dxl", 0, 2, 1, "s"),
     ("il", 0, 1024, 1536, "s"),
+    ("pq", "x", 0, 0),
+    ("dxl", 0, 3, 0, "s"),
+    ("dxl", 0, 3, 1, "s"),
+    ("pt", "x", 1, 1, 1, "m3"),
+    ("pt", "x", 1, 1, 0, "m1"),
+    ("tq", 1, 0, 384),
+    ("pc", "x", 1, 1, 1, "s"),
+    ("lift", 6),
+    ("pc", "x", 1, 1, 0, "s"),
+    ("dw", 0, 0, "m5"),
+    ("dw", 1, 0, "m2"),
+    ("pq", "x", 1, 1),
     ("prod", 6),
-    ("dw", 1, 0),
-    ("dw", 1, 1),
+    ("dw", 2, 0, "m2"),
     ("tr", 0, (0, 1)),
-    ("dw", 0, 0),
-    ("coef", 7),
-    ("il", 1, 384, 768, "v"),
-    ("fc", 0, (0, 1), "s"),
-    ("dw", 0, 1),
-    ("dwl", 1, 0, "s"),
-    ("comb", 6),
-    ("dw", 2, 1),
-    ("fc", 0, (2, 3), "s"),
-    ("dw", 2, 0),
-    ("dwl", 1, 1, "s"),
-    ("tq", 1, 384, 768),
-    ("tr", 1, (2, 3)),
-    ("dwl", 2, 0, "s"),
-    ("fq", 0, (0, 1, 2, 3)),
-    ("dwl", 2, 1, "s"),
-    ("tr", 1, (0, 1)),
-    ("tq", 0, 1024, 1536),
-    ("dw", 3, 1),
-    ("fc", 1, (2, 3), "s"),
-    ("fc", 1, (0, 1), "v"),
     ("dwl", 0, 0, "s"),
-    ("dw", 3, 0),
-    ("il", 1, 768, 1152, "v"),
+    ("dwl", 1, 0, "s"),
+    ("il", 1, 384, 768, "s"),
+    ("tq", 1, 384, 768),
+    ("dw", 0, 1, "m4"),
     ("dwl", 0, 1, "s"),
-    ("dw", 4, 1),
-    ("dwl", 3, 0, "s"),
-    ("dw", 4, 0),
-    ("fq", 1, (0, 1, 2, 3)),
-    ("dwl", 3, 1, "s"),
-    ("dw", 5, 0),
-    ("tq", 1, 768, 1152),
-    ("dwl", 4, 0, "s"),
-    ("dw", 6, 0),
-    ("coef", 8),
+    ("dw", 1, 1, "m5"),
+    ("dw", 2, 1, "m0"),
+    ("dw", 4, 0, "m1"),
+    ("plain", 6, "s"),
+    ("dw", 3, 1, "m4"),
+    ("comb", 6),
     ("lift", 7),
-    ("dwl", 4, 1, "s"),
-    ("dw", 5, 1),
-    ("dwl", 5, 0, "s"),
-    ("dw", 7, 0),
+    ("dwl", 2, 0, "s"),
+    ("dwl", 2, 1, "s"),
+    ("il", 1, 768, 1152, "v"),
+    ("dwl", 1, 1, "s"),
     ("lift", 8, True),
-    ("plain", 7),
-    ("prod", 7),
-    ("dw", 7, 1),
-    ("dwl", 6, 0, "s"),
-    ("dw", 6, 1),
+    ("fc", 0, (2, 3), "s"),
+    ("fc", 0, (0, 1), "s"),
+    ("dw", 5, 0, "m3"),
+    ("dw", 3, 0, "m2"),
+    ("dwl", 3, 0, "s"),
+    ("dwl", 3, 1, "s"),
+    ("tq", 1, 768, 1152),
+    ("dw", 4, 1, "m5"),
+    ("tr", 1, (0, 1)),
+    ("plain", 7, "s"),
+    ("tq", 0, 1024, 1536),
+    ("tr", 1, (2, 3)),
+    ("fq", 0, (0, 1, 2, 3)),
+    ("dwl", 4, 0, "s"),
+    ("dw", 5, 1, "m4"),
+    ("dwl", 5, 0, "s"),
+    ("dw", 7, 1, "m2"),
+    ("dwl", 4, 1, "s"),
+    ("dw", 6, 0, "m1"),
+    ("fc", 1, (0, 1), "s"),
     ("dwl", 5, 1, "s"),
-    ("prod", 8),
-    ("dw", 8, 0),
+    ("fc", 1, (2, 3), "s"),
+    ("dw", 7, 0, "m5"),
     ("dwl", 7, 0, "s"),
-    ("comb", 7),
-    ("dw", 8, 1),
+    ("dw", 6, 1, "m4"),
+    ("dwl", 6, 0, "s"),
     ("dwl", 6, 1, "s"),
-    ("comb", 8),
-    ("coef", 10),
-    ("il", 1, 1152, 1344, "v"),
-    ("tr", 2, (0,)),
-    ("dwl", 7, 1, "s"),
-    ("fc", 2, (0,), "v"),
+    ("prod", 7),
+    ("dw", 8, 0, "m0"),
+    ("fq", 1, (0, 1, 2, 3)),
+    ("dx", 1, 1, 0, (0, 1), "m3"),
+    ("dx", 1, 0, 1, (0, 1), "m1"),
     ("dwl", 8, 0, "s"),
-    ("tq", 1, 1152, 1344),
-    ("dw", 9, 1),
-    ("fq", 2, (0,)),
-    ("dwl", 8, 1, "s"),
-    ("coef", 9),
-    ("coef", 11),
-    ("lift", 10, True),
-    ("dx", 1, 0, 1, (0, 1, 2)),
+    ("comb", 7),
+    ("il", 1, 1152, 1344, "s"),
+    ("prod", 8),
     ("lift", 9, True),
-    ("prod", 10),
-    ("dx", 1, 0, 0, (0, 1, 2)),
+    ("tq", 1, 1152, 1344),
+    ("comb", 8),
     ("prod", 9),
-    ("comb", 10),
-    ("lift", 11, True),
-    ("tr", 2, (2,)),
+    ("dx", 1, 0, 0, (0, 1), "m0"),
     ("comb", 9),
-    ("dxl", 1, 0, 0, "s"),
-    ("dxl", 1, 0, 1, "v"),
-    ("tr", 2, (1,)),
-    ("dw", 9, 0),
-    ("fc", 2, (2,), "v"),
-    ("fc", 2, (1,), "s"),
-    ("prod", 11),
-    ("fq", 2, (2,)),
-    ("dx", 1, 2, 0, (0, 1, 2)),
+    ("dw", 8, 1, "m4"),
+    ("dwl", 7, 1, "s"),
+    ("dw", 9, 0, "m5"),
     ("dwl", 9, 0, "s"),
-    ("dwl", 9, 1, "v"),
-    ("comb", 11),
-    ("dx", 1, 2, 1, (0, 1, 2)),
-    ("fq", 2, (1,)),
-    ("dxl", 1, 2, 0, "v"),
-    ("dx", 1, 1, 1, (0, 1, 2)),
     ("il", 1, 1344, 1536, "v"),
-    ("dxl", 1, 2, 1, "s"),
+    ("dw", 9, 1, "m2"),
+    ("dwl", 9, 1, "s"),
+    ("tr", 2, (0, 1)),
+    ("fc", 2, (0, 1), "s"),
+    ("tr", 2, (2, 3)),
+    ("dx", 1, 1, 1, (0, 1), "m5"),
+    ("fq", 2, (0, 1)),
+    ("dx", 1, 1, 0, (2,)),
+    ("dwl", 8, 1, "s"),
     ("tq", 1, 1344, 1536),
-    ("dx", 1, 1, 0, (0, 1, 2)),
-    ("tr", 2, (3,)),
-    ("dxl", 1, 1, 0, "v"),
+    ("fc", 2, (2, 3), "s"),
+    ("dx", 1, 1, 1, (2,)),
+    ("dxl", 1, 1, 0, "s"),
     ("dxl", 1, 1, 1, "s"),
-    ("dw", 10, 0),
-    ("fc", 2, (3,), "v"),
-    ("dw", 10, 1),
-    ("fq", 2, (3,)),
-    ("dwl", 10, 0, "v"),
-    ("dx", 1, 3, 1, (0, 1, 2)),
-    ("dwl", 10, 1, "v"),
-    ("dx", 1, 3, 0, (0, 1, 2)),
-    ("dw", 11, 1),
-    ("dxl", 1, 3, 0, "s"),
-    ("dxl", 1, 3, 1, "v"),
-    ("dw", 11, 0),
+    ("dw", 10, 0, "m4"),
+    ("dwl", 10, 0, "s"),
+    ("dw", 10, 1, "m2"),
+    ("dx", 1, 0, 1, (2,)),
+    ("dwl", 10, 1, "s"),
+    ("dx", 1, 0, 0, (2,)),
+    ("dxl", 1, 0, 0, "s"),
+    ("dxl", 1, 0, 1, "s"),
+    ("dw", 11, 0, "m5"),
+    ("dw", 11, 1, "m2"),
     ("dwl", 11, 0, "s"),
-    ("dwl", 11, 1, "v"),
+    ("dwl", 11, 1, "s"),
+    ("fq", 2, (2, 3)),
+    ("dx", 1, 2, 0, (0, 1, 2), "m3"),
+    ("dxl", 1, 2, 0, "s"),
+    ("dx", 1, 2, 1, (0, 1, 2), "m1"),
+    ("dx", 1, 3, 0, (0, 1, 2), "m2"),
+    ("dxl", 1, 2, 1, "s"),
+    ("dx", 1, 3, 1, (0, 1, 2), "m5"),
+    ("dxl", 1, 3, 0, "s"),
+    ("dxl", 1, 3, 1, "s"),
 ]
 
 
@@ -314,7 +309,7 @@ def tile_lorentzmla_pb_v_kernel(tc, x, freqs_cos, freqs_sin, wq_w, wq_b, q_rot, 
         raw_of = {}
 
         def load_raw(key, src):
-            raw = pool.tile([P, PACK, DIM], BF16, name="raw", bufs=3)
+            raw = pool.tile([P, PACK, DIM], BF16, name="raw", bufs=4)
             nc.sync.dma_start(out=raw[:], in_=src.rearrange("(p j) d -> p j d", j=PACK))
             raw_of[key] = raw
 
@@ -365,21 +360,20 @@ def tile_lorentzmla_pb_v_kernel(tc, x, freqs_cos, freqs_sin, wq_w, wq_b, q_rot, 
                  keep.tile([P, PACK, J], BF16, name="da1", align_bytes=64)]
 
         st = {}
+        copier = {"s": nc.scalar.copy, "v": nc.vector.tensor_copy}
 
-        def coef(u):
-            b, h0, nh, js = UNITS[u]
-            j0, nj = js[0], len(js)
-            g_t, go, jb = g_of[(b, h0, j0)]
-            c = pool.tile([P, nj, nh], F32, name="c", bufs=3)
-            g0 = g_t[:, j0 - jb:j0 - jb + nj, go:go + nh * DG].rearrange("p j (h d) -> p j h d", d=DG)[:, :, :, 0]
-            nc.vector.tensor_tensor(out=c[:], in0=g0, in1=rt[:, b, j0:j0 + nj, h0:h0 + nh], op=MULT)
-            st[("c", u)] = c
+        def coef(b, j0, nj):
+            g_t, go, jb = g_of[(b, 0, j0)]
+            c = pool.tile([P, nj, H], F32, name="c%d" % nj, bufs=2 if nj == 1 else 1)
+            g0 = g_t[:, j0 - jb:j0 - jb + nj, :].rearrange("p j (h d) -> p j h d", d=DG)[:, :, :, 0]
+            nc.vector.tensor_tensor(out=c[:], in0=g0, in1=rt[:, b, j0:j0 + nj, :], op=MULT)
+            for j in range(nj):
+                st[("c", b, j0 + j)] = c[:, j, :]
 
         def lift(u, direct=False):
             b, h0, nh, js = UNITS[u]
             j0, nj = js[0], len(js)
-            c = st[("c", u)]
-            dr = pool.tile([P, nj, nh, D], F32, name="dr", bufs=3)
+            dr = pool.tile([P, nj, nh, D], F32, name="dr", bufs=2)
             st[("dr", u)] = dr
             for j in js:
                 for h in range(nh):
@@ -389,15 +383,18 @@ def tile_lorentzmla_pb_v_kernel(tc, x, freqs_cos, freqs_sin, wq_w, wq_b, q_rot, 
                     parts = [(da_of[b][:, j, (h0 + h) * D:(h0 + h) * D + NOPE], 0, NOPE), (dr[:, j - j0, h, NOPE:D], NOPE, D)] if direct else [(dr[:, j - j0, h, :], 0, D)]
                     for (o, lo, hi) in parts:
                         nc.vector.scalar_tensor_tensor(
-                            out=o, in0=q_t[:, j - jb, qo + lo:qo + hi], scalar=c[:, j - j0, h:h + 1],
+                            out=o, in0=q_t[:, j - jb, qo + lo:qo + hi], scalar=st[("c", b, j)][:, h0 + h:h0 + h + 1],
                             in1=g[:, lo:hi], op0=MULT, op1=ADD)
 
-        def plain_part(u):
+        def plain_part(u, eng):
             b, h0, nh, js = UNITS[u]
             j0, nj = js[0], len(js)
             dr = st[("dr", u)]
-            nc.scalar.copy(out=da_of[b][:, j0:j0 + nj, h0 * D:(h0 + nh) * D].rearrange("p j (h d) -> p j h d", d=D)[:, :, :, 0:NOPE],
-                           in_=dr[:, :, :, 0:NOPE])
+            dst = da_of[b][:, j0:j0 + nj, h0 * D:(h0 + nh) * D].rearrange("p j (h d) -> p j h d", d=D)[:, :, :, 0:NOPE]
+            if eng == "g":
+                nc.gpsimd.tensor_scalar(out=dst, in0=dr[:, :, :, 0:NOPE], scalar1=1.0, scalar2=0.0, op0=MULT, op1=ADD)
+            else:
+                copier[eng](out=dst, in_=dr[:, :, :, 0:NOPE])
 
         def products(u):
             b, h0, nh, js = UNITS[u]
@@ -431,12 +428,9 @@ def tile_lorentzmla_pb_v_kernel(tc, x, freqs_cos, freqs_sin, wq_w, wq_b, q_rot, 
         def words_of(tile, pat):
             return tile[:].rearrange(pat).bitcast(F32)
 
-        copier = {"s": nc.scalar.copy, "v": nc.vector.tensor_copy}
-        banks = [0]
 
-        def new_bank(shape, dt):
-            banks[0] += 1
-            return psum.tile(shape, dt, name="m%d" % (banks[0] % NBANK))
+        def new_bank(shape, dt, bank):
+            return psum.tile(shape, dt, name=bank)
 
         def turn(eng, out, src):
             if eng == "g":
@@ -495,9 +489,9 @@ def tile_lorentzmla_pb_v_kernel(tc, x, freqs_cos, freqs_sin, wq_w, wq_b, q_rot, 
             c = slice(js[0] * P, (js[0] + len(js)) * P)
             nc.vector.quantize_mx(out=fcd[:, g, c].bitcast(E5), scales=fsc[:, g, c], in_=st[("fi", g)][:, c, :].rearrange("p n t -> p (n t)"))
 
-        def piece_turn(kind, g, n, k):
+        def piece_turn(kind, g, n, k, bank):
             raw = raw_of[(kind, g)]
-            pb = new_bank([P, 2, NT], BF16)
+            pb = new_bank([P, 2, NT], BF16, bank)
             st[("pb", kind, g, n, k)] = pb
             for v in range(2):
                 c0 = n * NT + (2 * k + v) * P
@@ -517,8 +511,8 @@ def tile_lorentzmla_pb_v_kernel(tc, x, freqs_cos, freqs_sin, wq_w, wq_b, q_rot, 
             c = slice(n * NT, (n + 1) * NT)
             nc.vector.quantize_mx(out=codes[:, g, c].bitcast(E4), scales=scales[:, g, c], in_=st[("stage", kind, g, n)][:].rearrange("p n t -> p (n t)"))
 
-        def dw_multiply(f, n):
-            acc = new_bank([P, NT], F32)
+        def dw_multiply(f, n, bank):
+            acc = new_bank([P, NT], F32, bank)
             st[("dw", f, n)] = acc
             r, c = slice(f * P, (f + 1) * P), slice(n * NT, (n + 1) * NT)
             for b in range(B):
@@ -531,9 +525,9 @@ def tile_lorentzmla_pb_v_kernel(tc, x, freqs_cos, freqs_sin, wq_w, wq_b, q_rot, 
                 return fc0[:, c], fs0[:, c]
             return fcd[:, g, j * P:(j + 1) * P], fsc[:, g, j * P:(j + 1) * P]
 
-        def dx_multiply(b, j, n, passes):
+        def dx_multiply(b, j, n, passes, bank=None):
             if passes[0] == 0:
-                st[("dx", b, j, n)] = new_bank([P, NT], F32)
+                st[("dx", b, j, n)] = new_bank([P, NT], F32, bank)
             c = slice(n * NT, (n + 1) * NT)
             for g in passes:
                 codes, scales = dx_codes(b, j, g)
@@ -541,6 +535,8 @@ def tile_lorentzmla_pb_v_kernel(tc, x, freqs_cos, freqs_sin, wq_w, wq_b, q_rot, 
                                     rhs=wc[:, g, c].bitcast(E4), rhs_scale=ws[:, g, c], start=(g == 0), stop=(g == NPASS_J - 1))
 
         def leave(key, n, eng, dst):
+            if key not in left and len(left) >= 8 and len(left) % 2 == 1:
+                st[("o",) + key] = pool.tile([P, DIM], F32, name="raw", bufs=4)
             o = tile_of(("o",) + key, [P, DIM], F32, "o", 4)
             copier[eng](out=o[:, n * NT:(n + 1) * NT], in_=st[key + (n,)][:])
             left[key] = left.get(key, 0) + 1

@@ -32,230 +32,222 @@ NBANK = 5
 PLAN = [
     ("coef", 0, 0, 1),
     ("lift", 0),
-    ("pt", "w", 0, 1, 0, "m2"),
-    ("pc", "w", 0, 1, 0, "s"),
-    ("prod", 0),
     ("coef", 0, 1, 1),
-    ("lift", 1),
-    ("plain", 1, "s"),
-    ("pt", "w", 0, 0, 0, "m2"),
     ("plain", 0, "s"),
+    ("prod", 0),
+    ("lift", 1),
+    ("pt", "w", 0, 0, 0, "m0"),
+    ("pt", "w", 0, 0, 1, "m1"),
+    ("pt", "w", 0, 1, 0, "m2"),
     ("comb", 0),
-    ("st", 0, 0, 2),
-    ("coef", 0, 2, 1),
+    ("plain", 1, "s"),
+    ("pt", "w", 0, 1, 1, "m3"),
     ("pc", "w", 0, 0, 0, "s"),
+    ("coef", 0, 2, 1),
     ("prod", 1),
-    ("pt", "w", 1, 1, 0, "m5"),
-    ("st", 0, 2, 1),
-    ("sc", 0, 0, 2, "s"),
-    ("lift", 2),
-    ("comb", 1),
-    ("pt", "w", 0, 1, 1, "m1"),
-    ("coef", 0, 3, 1),
-    ("pc", "w", 0, 1, 1, "s"),
-    ("plain", 2, "s"),
-    ("prod", 2),
-    ("pt", "w", 1, 1, 1, "m4"),
-    ("pc", "w", 1, 1, 1, "s"),
-    ("st", 1, 2, 1),
-    ("pt", "w", 0, 0, 1, "m2"),
-    ("pt", "w", 1, 0, 0, "m3"),
-    ("pc", "w", 1, 1, 0, "s"),
-    ("pt", "w", 2, 0, 1, "m5"),
-    ("pt", "w", 2, 1, 0, "m4"),
-    ("pq", "w", 0, 1),
-    ("comb", 2),
-    ("sc", 1, 2, 1, "s"),
+    ("st", 0, 0, 2),
     ("pc", "w", 0, 0, 1, "s"),
-    ("pq", "w", 0, 0),
-    ("pt", "w", 2, 0, 0, "m1"),
-    ("pc", "w", 1, 0, 0, "s"),
+    ("st", 0, 2, 1),
+    ("pc", "w", 0, 1, 0, "s"),
+    ("pc", "w", 0, 1, 1, "s"),
+    ("pt", "w", 1, 0, 0, "m4"),
+    ("sc", 0, 0, 2, "s"),
     ("sc", 0, 2, 1, "s"),
-    ("sq", 0),
-    ("pt", "w", 1, 0, 1, "m3"),
-    ("st", 2, 2, 1),
-    ("sc", 2, 2, 1, "s"),
-    ("lift", 3),
-    ("st", 1, 0, 2),
-    ("sc", 1, 0, 2, "s"),
-    ("pq", "w", 1, 1),
+    ("pq", "w", 0, 0),
+    ("pt", "w", 1, 0, 1, "m0"),
+    ("lift", 2),
+    ("pt", "w", 1, 1, 0, "m1"),
+    ("pc", "w", 1, 0, 0, "s"),
     ("pc", "w", 1, 0, 1, "s"),
-    ("coef", 1, 0, 4),
-    ("st", 2, 0, 2),
-    ("pt", "w", 2, 1, 1, "m0"),
-    ("prod", 3),
-    ("pc", "w", 2, 1, 0, "s"),
-    ("sc", 2, 0, 2, "s"),
-    ("pc", "w", 2, 0, 1, "s"),
-    ("pc", "w", 2, 1, 1, "s"),
+    ("pt", "w", 1, 1, 1, "m2"),
+    ("pq", "w", 0, 1),
+    ("plain", 2, "s"),
+    ("pc", "w", 1, 1, 0, "s"),
+    ("comb", 1),
+    ("pc", "w", 1, 1, 1, "s"),
+    ("coef", 0, 3, 1),
+    ("prod", 2),
+    ("st", 1, 0, 2),
+    ("st", 1, 2, 1),
+    ("pt", "w", 2, 0, 0, "m3"),
+    ("sc", 1, 0, 2, "s"),
+    ("sc", 1, 2, 1, "s"),
+    ("pt", "w", 2, 0, 1, "m4"),
     ("pc", "w", 2, 0, 0, "s"),
     ("pq", "w", 1, 0),
+    ("pc", "w", 2, 0, 1, "s"),
+    ("pq", "w", 1, 1),
+    ("lift", 3),
+    ("pd", "w", 2, 1, 0, "s"),
+    ("pd", "w", 2, 1, 1, "s"),
+    ("sq", 0),
     ("plain", 3, "s"),
+    ("comb", 2),
+    ("prod", 3),
+    ("pd", "x", 0, 0, 0, "s"),
+    ("st", 2, 0, 2),
+    ("st", 2, 2, 1),
+    ("pd", "x", 0, 0, 1, "s"),
+    ("sc", 2, 0, 2, "s"),
+    ("sc", 2, 2, 1, "s"),
     ("pq", "w", 2, 0),
-    ("dx", 0, 0, 0, (0, 1, 2), "m5"),
-    ("pd", "x", 0, 1, 1, "s"),
-    ("pt", "x", 0, 0, 1, "m1"),
-    ("dxl", 0, 0, 0, "s"),
-    ("comb", 3),
-    ("il", 0, 0, 512, "s"),
-    ("pt", "x", 1, 0, 0, "m5"),
-    ("sq", 1),
-    ("dx", 0, 1, 0, (0, 1, 2), "m2"),
     ("pd", "x", 0, 1, 0, "s"),
-    ("dxl", 0, 1, 0, "s"),
-    ("lift", 4),
-    ("plain", 4, "s"),
-    ("lift", 5),
-    ("plain", 5, "s"),
     ("pq", "w", 2, 1),
-    ("dx", 0, 0, 1, (0, 1, 2), "m4"),
+    ("sq", 1),
+    ("pd", "x", 0, 1, 1, "s"),
+    ("coef", 1, 0, 4),
+    ("lift", 4),
+    ("dx", 0, 0, 0, (0, 1, 2), "m1"),
+    ("dx", 0, 0, 1, (0, 1, 2), "m2"),
+    ("dx", 0, 1, 0, (0, 1, 2), "m3"),
+    ("pd", "x", 1, 0, 0, "s"),
+    ("sq", 2),
+    ("pd", "x", 1, 0, 1, "s"),
+    ("plain", 4, "s"),
+    ("dx", 0, 1, 1, (0, 1, 2), "m4"),
+    ("comb", 3),
+    ("dxl", 0, 0, 0, "s"),
     ("dxl", 0, 0, 1, "s"),
     ("prod", 4),
-    ("prod", 5),
-    ("dx", 0, 1, 1, (0, 1, 2), "m3"),
-    ("dxl", 0, 1, 1, "s"),
-    ("pc", "x", 0, 0, 1, "s"),
-    ("sq", 2),
-    ("comb", 4),
-    ("tq", 0, 0, 512),
-    ("pt", "x", 1, 0, 1, "m4"),
-    ("pc", "x", 1, 0, 1, "s"),
-    ("comb", 5),
     ("st", 3, 0, 2),
+    ("dxl", 0, 1, 0, "s"),
     ("st", 3, 2, 1),
+    ("dxl", 0, 1, 1, "s"),
     ("sc", 3, 0, 2, "s"),
     ("sc", 3, 2, 1, "s"),
-    ("il", 0, 512, 1024, "s"),
-    ("sq", 3),
-    ("pt", "x", 0, 0, 0, "m1"),
-    ("il", 1, 0, 384, "v"),
-    ("dx", 0, 2, 0, (0, 1, 2), "m0"),
-    ("dxl", 0, 2, 0, "s"),
-    ("dx", 0, 2, 1, (0, 1, 2), "m0"),
-    ("pc", "x", 0, 0, 0, "s"),
-    ("pq", "x", 0, 1),
-    ("dx", 0, 3, 1, (0, 1, 2), "m4"),
-    ("dx", 0, 3, 0, (0, 1, 2), "m5"),
-    ("pc", "x", 1, 0, 0, "s"),
-    ("tq", 0, 512, 1024),
-    ("pq", "x", 1, 0),
-    ("tr", 0, (2, 3)),
-    ("dxl", 0, 2, 1, "s"),
-    ("il", 0, 1024, 1536, "s"),
     ("pq", "x", 0, 0),
+    ("dx", 0, 2, 0, (0, 1, 2), "m2"),
+    ("pd", "x", 1, 1, 0, "s"),
+    ("il", 0, 0, 512, "s"),
+    ("pq", "x", 1, 0),
+    ("pd", "x", 1, 1, 1, "s"),
+    ("dx", 0, 2, 1, (0, 1, 2), "m3"),
+    ("lift", 5),
+    ("sq", 3),
+    ("plain", 5, "s"),
+    ("dxl", 0, 2, 0, "s"),
+    ("comb", 4),
+    ("dx", 0, 3, 0, (0, 1, 2), "m4"),
+    ("dxl", 0, 2, 1, "s"),
+    ("il", 0, 512, 1024, "s"),
+    ("il", 1, 0, 384, "v"),
+    ("dx", 0, 3, 1, (0, 1, 2), "m0"),
+    ("prod", 5),
     ("dxl", 0, 3, 0, "s"),
     ("dxl", 0, 3, 1, "s"),
-    ("pt", "x", 1, 1, 1, "m3"),
-    ("pt", "x", 1, 1, 0, "m1"),
-    ("tq", 1, 0, 384),
-    ("pc", "x", 1, 1, 1, "s"),
-    ("lift", 6),
-    ("pc", "x", 1, 1, 0, "s"),
-    ("dw", 0, 0, "m5"),
-    ("dw", 1, 0, "m2"),
     ("pq", "x", 1, 1),
-    ("prod", 6),
-    ("dw", 2, 0, "m2"),
-    ("tr", 0, (0, 1)),
+    ("il", 0, 1024, 1536, "s"),
+    ("pq", "x", 0, 1),
+    ("tq", 0, 0, 512),
+    ("tq", 1, 0, 384),
+    ("lift", 6),
+    ("dw", 0, 0, "m1"),
+    ("dw", 0, 1, "m2"),
     ("dwl", 0, 0, "s"),
-    ("dwl", 1, 0, "s"),
-    ("il", 1, 384, 768, "s"),
-    ("tq", 1, 384, 768),
-    ("dw", 0, 1, "m4"),
+    ("dw", 1, 0, "m3"),
     ("dwl", 0, 1, "s"),
-    ("dw", 1, 1, "m5"),
-    ("dw", 2, 1, "m0"),
-    ("dw", 4, 0, "m1"),
+    ("dw", 1, 1, "m4"),
+    ("tq", 0, 512, 1024),
     ("plain", 6, "s"),
-    ("dw", 3, 1, "m4"),
-    ("comb", 6),
-    ("lift", 7),
-    ("dwl", 2, 0, "s"),
-    ("dwl", 2, 1, "s"),
-    ("il", 1, 768, 1152, "v"),
+    ("dwl", 1, 0, "s"),
+    ("dw", 2, 0, "m0"),
+    ("comb", 5),
     ("dwl", 1, 1, "s"),
-    ("lift", 8, True),
-    ("fc", 0, (2, 3), "s"),
+    ("dw", 2, 1, "m1"),
+    ("il", 1, 384, 768, "v"),
+    ("tr", 0, (0, 1)),
+    ("dwl", 2, 0, "s"),
+    ("prod", 6),
+    ("dwl", 2, 1, "s"),
+    ("tr", 0, (2, 3)),
     ("fc", 0, (0, 1), "s"),
-    ("dw", 5, 0, "m3"),
+    ("fc", 0, (2, 3), "s"),
+    ("tq", 1, 384, 768),
+    ("fq", 0, (0, 1, 2, 3)),
     ("dw", 3, 0, "m2"),
+    ("lift", 7),
+    ("dw", 3, 1, "m3"),
     ("dwl", 3, 0, "s"),
     ("dwl", 3, 1, "s"),
-    ("tq", 1, 768, 1152),
-    ("dw", 4, 1, "m5"),
-    ("tr", 1, (0, 1)),
-    ("plain", 7, "s"),
+    ("dw", 4, 0, "m4"),
     ("tq", 0, 1024, 1536),
-    ("tr", 1, (2, 3)),
-    ("fq", 0, (0, 1, 2, 3)),
+    ("plain", 7, "s"),
+    ("dw", 4, 1, "m0"),
     ("dwl", 4, 0, "s"),
-    ("dw", 5, 1, "m4"),
-    ("dwl", 5, 0, "s"),
-    ("dw", 7, 1, "m2"),
+    ("dw", 5, 0, "m1"),
+    ("comb", 6),
     ("dwl", 4, 1, "s"),
-    ("dw", 6, 0, "m1"),
-    ("fc", 1, (0, 1), "s"),
-    ("dwl", 5, 1, "s"),
-    ("fc", 1, (2, 3), "s"),
-    ("dw", 7, 0, "m5"),
-    ("dwl", 7, 0, "s"),
-    ("dw", 6, 1, "m4"),
-    ("dwl", 6, 0, "s"),
-    ("dwl", 6, 1, "s"),
+    ("dw", 5, 1, "m2"),
+    ("il", 1, 768, 1152, "v"),
+    ("dwl", 5, 0, "s"),
     ("prod", 7),
-    ("dw", 8, 0, "m0"),
+    ("tr", 1, (0, 1)),
+    ("dwl", 5, 1, "s"),
+    ("tr", 1, (2, 3)),
+    ("fc", 1, (0, 1), "s"),
+    ("fc", 1, (2, 3), "s"),
     ("fq", 1, (0, 1, 2, 3)),
-    ("dx", 1, 1, 0, (0, 1), "m3"),
-    ("dx", 1, 0, 1, (0, 1), "m1"),
-    ("dwl", 8, 0, "s"),
+    ("lift", 8, True),
+    ("tq", 1, 768, 1152),
     ("comb", 7),
-    ("il", 1, 1152, 1344, "s"),
-    ("prod", 8),
-    ("lift", 9, True),
-    ("tq", 1, 1152, 1344),
-    ("comb", 8),
-    ("prod", 9),
+    ("dw", 6, 0, "m2"),
     ("dx", 1, 0, 0, (0, 1), "m0"),
-    ("comb", 9),
-    ("dw", 8, 1, "m4"),
-    ("dwl", 7, 1, "s"),
-    ("dw", 9, 0, "m5"),
-    ("dwl", 9, 0, "s"),
-    ("il", 1, 1344, 1536, "v"),
-    ("dw", 9, 1, "m2"),
-    ("dwl", 9, 1, "s"),
+    ("dx", 1, 0, 1, (0, 1), "m1"),
+    ("il", 1, 1152, 1344, "v"),
+    ("prod", 8),
+    ("dw", 6, 1, "m3"),
+    ("dwl", 6, 0, "s"),
+    ("dw", 7, 0, "m4"),
+    ("lift", 9, True),
+    ("dwl", 6, 1, "s"),
+    ("dw", 7, 1, "m2"),
+    ("comb", 8),
+    ("dwl", 7, 0, "s"),
+    ("prod", 9),
     ("tr", 2, (0, 1)),
+    ("dwl", 7, 1, "s"),
+    ("dw", 8, 0, "m3"),
+    ("tq", 1, 1152, 1344),
+    ("dw", 8, 1, "m4"),
     ("fc", 2, (0, 1), "s"),
-    ("tr", 2, (2, 3)),
-    ("dx", 1, 1, 1, (0, 1), "m5"),
+    ("comb", 9),
+    ("dwl", 8, 0, "s"),
     ("fq", 2, (0, 1)),
-    ("dx", 1, 1, 0, (2,)),
     ("dwl", 8, 1, "s"),
+    ("tr", 2, (2, 3)),
+    ("il", 1, 1344, 1536, "v"),
+    ("dx", 1, 1, 0, (0, 1), "m4"),
+    ("dw", 9, 0, "m2"),
+    ("dw", 9, 1, "m3"),
     ("tq", 1, 1344, 1536),
     ("fc", 2, (2, 3), "s"),
-    ("dx", 1, 1, 1, (2,)),
-    ("dxl", 1, 1, 0, "s"),
-    ("dxl", 1, 1, 1, "s"),
-    ("dw", 10, 0, "m4"),
-    ("dwl", 10, 0, "s"),
-    ("dw", 10, 1, "m2"),
-    ("dx", 1, 0, 1, (2,)),
-    ("dwl", 10, 1, "s"),
+    ("dx", 1, 1, 1, (0, 1), "m5"),
     ("dx", 1, 0, 0, (2,)),
-    ("dxl", 1, 0, 0, "s"),
-    ("dxl", 1, 0, 1, "s"),
-    ("dw", 11, 0, "m5"),
-    ("dw", 11, 1, "m2"),
-    ("dwl", 11, 0, "s"),
-    ("dwl", 11, 1, "s"),
+    ("dx", 1, 0, 1, (2,)),
+    ("dx", 1, 1, 0, (2,)),
+    ("dx", 1, 1, 1, (2,)),
+    ("dwl", 9, 0, "s"),
+    ("dw", 10, 0, "m2"),
+    ("dwl", 9, 1, "s"),
     ("fq", 2, (2, 3)),
-    ("dx", 1, 2, 0, (0, 1, 2), "m3"),
-    ("dxl", 1, 2, 0, "s"),
-    ("dx", 1, 2, 1, (0, 1, 2), "m1"),
-    ("dx", 1, 3, 0, (0, 1, 2), "m2"),
+    ("dxl", 1, 0, 0, "s"),
+    ("dw", 10, 1, "m3"),
+    ("dxl", 1, 0, 1, "v"),
+    ("dxl", 1, 1, 0, "v"),
+    ("dw", 11, 0, "m0"),
+    ("dwl", 10, 0, "v"),
+    ("dxl", 1, 1, 1, "s"),
+    ("dw", 11, 1, "m1"),
+    ("dwl", 10, 1, "s"),
+    ("dwl", 11, 0, "v"),
+    ("dwl", 11, 1, "s"),
+    ("dx", 1, 2, 0, (0, 1, 2), "m4"),
+    ("dx", 1, 2, 1, (0, 1, 2), "m5"),
+    ("dxl", 1, 2, 0, "v"),
     ("dxl", 1, 2, 1, "s"),
-    ("dx", 1, 3, 1, (0, 1, 2), "m5"),
-    ("dxl", 1, 3, 0, "s"),
+    ("dx", 1, 3, 0, (0, 1, 2), "m2"),
+    ("dx", 1, 3, 1, (0, 1, 2), "m3"),
+    ("dxl", 1, 3, 0, "v"),
     ("dxl", 1, 3, 1, "s"),
 ]
 
@@ -266,7 +258,6 @@ def tile_lorentzmla_pb_v_kernel(tc, x, freqs_cos, freqs_sin, wq_w, wq_b, q_rot, 
         keep = ctx.enter_context(tc.tile_pool(name="keep", bufs=1))
         pool = ctx.enter_context(tc.tile_pool(name="work", bufs=2))
         psum = ctx.enter_context(tc.psum_pool(name="psum", bufs=1))
-        ctx.enter_context(tc.manual_schedule())
 
         t_sb = keep.tile([P, B, PACK, H], F32, name="t_sb")
         nc.sync.dma_start(out=t_sb[:], in_=t.rearrange("b (p j) h o -> p b j (h o)", j=PACK))

from contextlib import ExitStack

import concourse.mybir as mybir
from concourse.masks import make_identity

B, S, DIM, H = 2, 512, 1024, 8
NOPE, ROPE = 64, 128
D = NOPE + ROPE
DG = D + 1
T, J = B * S, H * D
P = 128
PACK = 4
KP = P * PACK
NPASS_J = J // KP
NT = 512

FLOPS = 2 * 2 * T * J * DIM
BYTES = 2 * (T * DIM + 2 * S * 64 + J * DIM + T * H * DG) + 4 * (T * H * D + T * H + T * DIM + J * DIM)

F32 = mybir.dt.float32
BF16 = mybir.dt.bfloat16
U32 = mybir.dt.uint32
U8 = mybir.dt.uint8
E4 = mybir.dt.float8_e4m3fn_x4
E5 = mybir.dt.float8_e5m2_x4
ADD = mybir.AluOpType.add
MULT = mybir.AluOpType.mult

SLOTS = (0, 1, 2, 3)
UNITS = [(0, 0, 8, (0,)), (0, 0, 8, (1,)), (0, 0, 8, (2,)), (0, 0, 8, (3,)), (1, 0, 2, SLOTS), (1, 2, 2, SLOTS), (1, 4, 2, SLOTS), (1, 6, 1, SLOTS), (1, 7, 1, (0, 1)), (1, 7, 1, (2, 3))]
NBANK = 5
PLAN = [
    ("coef", 0, 0, 1),
    ("lift", 0),
    ("coef", 0, 1, 1),
    ("plain", 0, "s"),
    ("prod", 0),
    ("lift", 1),
    ("pt", "w", 0, 0, 0, "m0"),
    ("pt", "w", 0, 0, 1, "m1"),
    ("pt", "w", 0, 1, 0, "m2"),
    ("comb", 0),
    ("plain", 1, "s"),
    ("pt", "w", 0, 1, 1, "m3"),
    ("pc", "w", 0, 0, 0, "s"),
    ("coef", 0, 2, 1),
    ("prod", 1),
    ("st", 0, 0, 2),
    ("pc", "w", 0, 0, 1, "s"),
    ("st", 0, 2, 1),
    ("pc", "w", 0, 1, 0, "s"),
    ("pc", "w", 0, 1, 1, "s"),
    ("pt", "w", 1, 0, 0, "m4"),
    ("sc", 0, 0, 2, "s"),
    ("sc", 0, 2, 1, "s"),
    ("pq", "w", 0, 0),
    ("pt", "w", 1, 0, 1, "m0"),
    ("lift", 2),
    ("pt", "w", 1, 1, 0, "m1"),
    ("pc", "w", 1, 0, 0, "s"),
    ("pc", "w", 1, 0, 1, "s"),
    ("pt", "w", 1, 1, 1, "m2"),
    ("pq", "w", 0, 1),
    ("plain", 2, "s"),
    ("pc", "w", 1, 1, 0, "s"),
    ("comb", 1),
    ("pc", "w", 1, 1, 1, "s"),
    ("coef", 0, 3, 1),
    ("prod", 2),
    ("st", 1, 0, 2),
    ("st", 1, 2, 1),
    ("pt", "w", 2, 0, 0, "m3"),
    ("sc", 1, 0, 2, "s"),
    ("sc", 1, 2, 1, "s"),
    ("pt", "w", 2, 0, 1, "m4"),
    ("pc", "w", 2, 0, 0, "s"),
    ("pq", "w", 1, 0),
    ("pc", "w", 2, 0, 1, "s"),
    ("pq", "w", 1, 1),
    ("lift", 3),
    ("pd", "w", 2, 1, 0, "s"),
    ("pd", "w", 2, 1, 1, "s"),
    ("sq", 0),
    ("plain", 3, "s"),
    ("comb", 2),
    ("prod", 3),
    ("pd", "x", 0, 0, 0, "s"),
    ("st", 2, 0, 2),
    ("st", 2, 2, 1),
    ("pd", "x", 0, 0, 1, "s"),
    ("sc", 2, 0, 2, "s"),
    ("sc", 2, 2, 1, "s"),
    ("pq", "w", 2, 0),
    ("pd", "x", 0, 1, 0, "s"),
    ("pq", "w", 2, 1),
    ("sq", 1),
    ("pd", "x", 0, 1, 1, "s"),
    ("coef", 1, 0, 4),
    ("lift", 4),
    ("dx", 0, 0, 0, (0, 1, 2), "m1"),
    ("dx", 0, 0, 1, (0, 1, 2), "m2"),
    ("dx", 0, 1, 0, (0, 1, 2), "m3"),
    ("pd", "x", 1, 0, 0, "s"),
    ("sq", 2),
    ("pd", "x", 1, 0, 1, "s"),
    ("plain", 4, "s"),
    ("dx", 0, 1, 1, (0, 1, 2), "m4"),
    ("comb", 3),
    ("dxl", 0, 0, 0, "s"),
    ("dxl", 0, 0, 1, "s"),
    ("prod", 4),
    ("st", 3, 0, 2),
    ("dxl", 0, 1, 0, "s"),
    ("st", 3, 2, 1),
    ("dxl", 0, 1, 1, "s"),
    ("sc", 3, 0, 2, "s"),
    ("sc", 3, 2, 1, "s"),
    ("pq", "x", 0, 0),
    ("dx", 0, 2, 0, (0, 1, 2), "m2"),
    ("pd", "x", 1, 1, 0, "s"),
    ("il", 0, 0, 512, "s"),
    ("pq", "x", 1, 0),
    ("pd", "x", 1, 1, 1, "s"),
    ("dx", 0, 2, 1, (0, 1, 2), "m3"),
    ("lift", 5),
    ("sq", 3),
    ("plain", 5, "s"),
    ("dxl", 0, 2, 0, "s"),
    ("comb", 4),
    ("dx", 0, 3, 0, (0, 1, 2), "m4"),
    ("dxl", 0, 2, 1, "s"),
    ("il", 0, 512, 1024, "s"),
    ("il", 1, 0, 384, "v"),
    ("dx", 0, 3, 1, (0, 1, 2), "m0"),
    ("prod", 5),
    ("dxl", 0, 3, 0, "s"),
    ("dxl", 0, 3, 1, "s"),
    ("pq", "x", 1, 1),
    ("il", 0, 1024, 1536, "s"),
    ("pq", "x", 0, 1),
    ("tq", 0, 0, 512),
    ("tq", 1, 0, 384),
    ("lift", 6),
    ("dw", 0, 0, "m1"),
    ("dw", 0, 1, "m2"),
    ("dwl", 0, 0, "s"),
    ("dw", 1, 0, "m3"),
    ("dwl", 0, 1, "s"),
    ("dw", 1, 1, "m4"),
    ("tq", 0, 512, 1024),
    ("plain", 6, "s"),
    ("dwl", 1, 0, "s"),
    ("dw", 2, 0, "m0"),
    ("comb", 5),
    ("dwl", 1, 1, "s"),
    ("dw", 2, 1, "m1"),
    ("il", 1, 384, 768, "v"),
    ("tr", 0, (0, 1)),
    ("dwl", 2, 0, "s"),
    ("prod", 6),
    ("dwl", 2, 1, "s"),
    ("tr", 0, (2, 3)),
    ("fc", 0, (0, 1), "s"),
    ("fc", 0, (2, 3), "s"),
    ("tq", 1, 384, 768),
    ("fq", 0, (0, 1, 2, 3)),
    ("dw", 3, 0, "m2"),
    ("lift", 7),
    ("dw", 3, 1, "m3"),
    ("dwl", 3, 0, "s"),
    ("dwl", 3, 1, "s"),
    ("dw", 4, 0, "m4"),
    ("tq", 0, 1024, 1536),
    ("plain", 7, "s"),
    ("dw", 4, 1, "m0"),
    ("dwl", 4, 0, "s"),
    ("dw", 5, 0, "m1"),
    ("comb", 6),
    ("dwl", 4, 1, "s"),
    ("dw", 5, 1, "m2"),
    ("il", 1, 768, 1152, "v"),
    ("dwl", 5, 0, "s"),
    ("prod", 7),
    ("tr", 1, (0, 1)),
    ("dwl", 5, 1, "s"),
    ("tr", 1, (2, 3)),
    ("fc", 1, (0, 1), "s"),
    ("fc", 1, (2, 3), "s"),
    ("fq", 1, (0, 1, 2, 3)),
    ("lift", 8, True),
    ("tq", 1, 768, 1152),
    ("comb", 7),
    ("dw", 6, 0, "m2"),
    ("dx", 1, 0, 0, (0, 1), "m0"),
    ("dx", 1, 0, 1, (0, 1), "m1"),
    ("il", 1, 1152, 1344, "v"),
    ("prod", 8),
    ("dw", 6, 1, "m3"),
    ("dwl", 6, 0, "s"),
    ("dw", 7, 0, "m4"),
    ("lift", 9, True),
    ("dwl", 6, 1, "s"),
    ("dw", 7, 1, "m2"),
    ("comb", 8),
    ("dwl", 7, 0, "s"),
    ("prod", 9),
    ("tr", 2, (0, 1)),
    ("dwl", 7, 1, "s"),
    ("dw", 8, 0, "m3"),
    ("tq", 1, 1152, 1344),
    ("dw", 8, 1, "m4"),
    ("fc", 2, (0, 1), "s"),
    ("comb", 9),
    ("dwl", 8, 0, "s"),
    ("fq", 2, (0, 1)),
    ("dwl", 8, 1, "s"),
    ("tr", 2, (2, 3)),
    ("il", 1, 1344, 1536, "v"),
    ("dx", 1, 1, 0, (0, 1), "m4"),
    ("dw", 9, 0, "m2"),
    ("dw", 9, 1, "m3"),
    ("tq", 1, 1344, 1536),
    ("fc", 2, (2, 3), "s"),
    ("dx", 1, 1, 1, (0, 1), "m5"),
    ("dx", 1, 0, 0, (2,)),
    ("dx", 1, 0, 1, (2,)),
    ("dx", 1, 1, 0, (2,)),
    ("dx", 1, 1, 1, (2,)),
    ("dwl", 9, 0, "s"),
    ("dw", 10, 0, "m2"),
    ("dwl", 9, 1, "s"),
    ("fq", 2, (2, 3)),
    ("dxl", 1, 0, 0, "s"),
    ("dw", 10, 1, "m3"),
    ("dxl", 1, 0, 1, "v"),
    ("dxl", 1, 1, 0, "v"),
    ("dw", 11, 0, "m0"),
    ("dwl", 10, 0, "v"),
    ("dxl", 1, 1, 1, "s"),
    ("dw", 11, 1, "m1"),
    ("dwl", 10, 1, "s"),
    ("dwl", 11, 0, "v"),
    ("dwl", 11, 1, "s"),
    ("dx", 1, 2, 0, (0, 1, 2), "m4"),
    ("dx", 1, 2, 1, (0, 1, 2), "m5"),
    ("dxl", 1, 2, 0, "v"),
    ("dxl", 1, 2, 1, "s"),
    ("dx", 1, 3, 0, (0, 1, 2), "m2"),
    ("dx", 1, 3, 1, (0, 1, 2), "m3"),
    ("dxl", 1, 3, 0, "v"),
    ("dxl", 1, 3, 1, "s"),
]


def tile_lorentzmla_pb_v_kernel(tc, x, freqs_cos, freqs_sin, wq_w, wq_b, q_rot, t, grad_out, out_0, out_1):
    nc = tc.nc
    with ExitStack() as ctx:
        keep = ctx.enter_context(tc.tile_pool(name="keep", bufs=1))
        pool = ctx.enter_context(tc.tile_pool(name="work", bufs=2))
        psum = ctx.enter_context(tc.psum_pool(name="psum", bufs=1))

        t_sb = keep.tile([P, B, PACK, H], F32, name="t_sb")
        nc.sync.dma_start(out=t_sb[:], in_=t.rearrange("b (p j) h o -> p b j (h o)", j=PACK))
        q_of, g_of = {}, {}

        def load_slot_g(j):
            g_t = pool.tile([P, 1, H * DG], BF16, name="g2", bufs=2)
            nc.sync.dma_start(out=g_t[:, 0, :], in_=grad_out[0].rearrange("(p j) h d -> p j (h d)", j=PACK)[:, j, :])
            for h in range(H):
                g_of[(0, h, j)] = (g_t, h * DG, j)

        def load_slot_q(j, parts):
            q_t = pool.tile([P, 1, H * D], F32, name="q2", bufs=4)
            n = H * D // parts
            for i in range(parts):
                nc.sync.dma_start(out=q_t[:, 0, i * n:(i + 1) * n], in_=q_rot[0].rearrange("(p j) h d -> p j (h d)", j=PACK)[:, j, i * n:(i + 1) * n])
            for h in range(H):
                q_of[(0, h, j)] = (q_t, h * D, j)

        def load_g(b, h0, nh, bufs):
            g_t = pool.tile([P, PACK, nh * DG], BF16, name="g%d" % nh, bufs=bufs)
            src = grad_out[b].rearrange("(p j) h d -> p j (h d)", j=PACK)
            nc.sync.dma_start(out=g_t[:], in_=src[:, :, h0 * DG:(h0 + nh) * DG])
            for h in range(nh):
                for j in range(PACK):
                    g_of[(b, h0 + h, j)] = (g_t, h * DG, 0)

        def load_q(b, h0, nh, bufs, by_slot=False):
            q_t = pool.tile([P, PACK, nh * D], F32, name="q%d" % nh, bufs=bufs)
            src = q_rot[b].rearrange("(p j) h d -> p j (h d)", j=PACK)[:, :, h0 * D:(h0 + nh) * D]
            if by_slot:
                for j in range(PACK):
                    nc.sync.dma_start(out=q_t[:, j, :], in_=src[:, j, :])
            else:
                nc.sync.dma_start(out=q_t[:], in_=src)
            for h in range(nh):
                for j in range(PACK):
                    q_of[(b, h0 + h, j)] = (q_t, h * D, 0)

        raw_of = {}

        def load_raw(key, src):
            raw = pool.tile([P, PACK, DIM], BF16, name="raw", bufs=4)
            nc.sync.dma_start(out=raw[:], in_=src.rearrange("(p j) d -> p j d", j=PACK))
            raw_of[key] = raw

        load_slot_g(0)
        load_slot_q(0, 4)
        cs = keep.tile([P, 2, PACK * 64], BF16, name="cs")
        nc.sync.dma_start(out=cs[:, 0, :], in_=freqs_cos.rearrange("(p j) f -> p (j f)", j=PACK))
        nc.sync.dma_start(out=cs[:, 1, :], in_=freqs_sin.rearrange("(p j) f -> p (j f)", j=PACK))
        load_slot_g(1)
        load_slot_q(1, 1)
        load_raw(("w", 0), wq_w[0:KP, :])
        load_slot_g(2)
        load_slot_q(2, 1)
        load_raw(("w", 1), wq_w[KP:2 * KP, :])
        load_slot_g(3)
        load_slot_q(3, 1)
        load_raw(("w", 2), wq_w[2 * KP:3 * KP, :])
        load_g(1, 0, 8, 1)
        load_q(1, 0, 2, 4)
        load_raw(("x", 0), x[0])
        load_q(1, 2, 2, 4)
        load_raw(("x", 1), x[1])
        load_q(1, 4, 2, 4)
        load_q(1, 6, 2, 4)
        ident = keep.tile([P, P], F32, name="ident")
        make_identity(nc, ident[:])
        ident_b = keep.tile([P, P], BF16, name="ident_b")
        make_identity(nc, ident_b[:])
        tab = keep.tile([P, 2, PACK * 64, 2], BF16, name="tab")
        nc.scalar.copy(out=tab[:, 0, :, :], in_=cs[:, 0, :].unsqueeze(2).to_broadcast([P, PACK * 64, 2]))
        nc.scalar.activation(out=tab[:, 1, :, 0], in_=cs[:, 1, :], func=mybir.ActivationFunctionType.Copy, scale=-1.0)
        nc.scalar.copy(out=tab[:, 1, :, 1], in_=cs[:, 1, :])

        rt = keep.tile([P, B, PACK, H], F32, name="rt")
        nc.vector.reciprocal(out=rt[:], in_=t_sb[:])

        xc = keep.tile([P, B, DIM], U32, name="xc", align_bytes=64)
        xs = keep.tile([P, B, DIM], U8, name="xs", align_bytes=64)
        wc = keep.tile([P, NPASS_J, DIM], U32, name="wc", align_bytes=64)
        ws = keep.tile([P, NPASS_J, DIM], U8, name="ws", align_bytes=64)
        tcd = keep.tile([P, B, J], U32, name="tcd", align_bytes=64)
        tsc = keep.tile([P, B, J], U8, name="tsc", align_bytes=64)
        fc0 = keep.tile([P, S * NPASS_J], U32, name="fc0", align_bytes=64)
        fs0 = keep.tile([P, S * NPASS_J], U8, name="fs0", align_bytes=64)
        fcd = keep.tile([P, NPASS_J, S], U32, name="fcd", align_bytes=64)
        fsc = keep.tile([P, NPASS_J, S], U8, name="fsc", align_bytes=64)
        da_of = [keep.tile([P, PACK, J], BF16, name="da0", align_bytes=64),
                 keep.tile([P, PACK, J], BF16, name="da1", align_bytes=64)]

        st = {}
        copier = {"s": nc.scalar.copy, "v": nc.vector.tensor_copy}

        def coef(b, j0, nj):
            g_t, go, jb = g_of[(b, 0, j0)]
            c = pool.tile([P, nj, H], F32, name="c%d" % nj, bufs=2 if nj == 1 else 1)
            g0 = g_t[:, j0 - jb:j0 - jb + nj, :].rearrange("p j (h d) -> p j h d", d=DG)[:, :, :, 0]
            nc.vector.tensor_tensor(out=c[:], in0=g0, in1=rt[:, b, j0:j0 + nj, :], op=MULT)
            for j in range(nj):
                st[("c", b, j0 + j)] = c[:, j, :]

        def lift(u, direct=False):
            b, h0, nh, js = UNITS[u]
            j0, nj = js[0], len(js)
            dr = pool.tile([P, nj, nh, D], F32, name="dr", bufs=2)
            st[("dr", u)] = dr
            for j in js:
                for h in range(nh):
                    q_t, qo, jb = q_of[(b, h0 + h, j)]
                    g_t, go, jb = g_of[(b, h0 + h, j)]
                    g = g_t[:, j - jb, go + 1:go + DG]
                    parts = [(da_of[b][:, j, (h0 + h) * D:(h0 + h) * D + NOPE], 0, NOPE), (dr[:, j - j0, h, NOPE:D], NOPE, D)] if direct else [(dr[:, j - j0, h, :], 0, D)]
                    for (o, lo, hi) in parts:
                        nc.vector.scalar_tensor_tensor(
                            out=o, in0=q_t[:, j - jb, qo + lo:qo + hi], scalar=st[("c", b, j)][:, h0 + h:h0 + h + 1],
                            in1=g[:, lo:hi], op0=MULT, op1=ADD)

        def plain_part(u, eng):
            b, h0, nh, js = UNITS[u]
            j0, nj = js[0], len(js)
            dr = st[("dr", u)]
            dst = da_of[b][:, j0:j0 + nj, h0 * D:(h0 + nh) * D].rearrange("p j (h d) -> p j h d", d=D)[:, :, :, 0:NOPE]
            if eng == "g":
                nc.gpsimd.tensor_scalar(out=dst, in0=dr[:, :, :, 0:NOPE], scalar1=1.0, scalar2=0.0, op0=MULT, op1=ADD)
            else:
                copier[eng](out=dst, in_=dr[:, :, :, 0:NOPE])

        def products(u):
            b, h0, nh, js = UNITS[u]
            j0, nj = js[0], len(js)
            dr = st[("dr", u)]
            a = pool.tile([P, nj, nh, ROPE], F32, name="a", bufs=2)
            st[("a", u)] = a

            def table(k):
                v = tab[:, k, :, :].rearrange("p (j f) e -> p j (f e)", j=PACK)[:, j0:j0 + nj, :]
                return v.unsqueeze(2).to_broadcast([P, nj, nh, ROPE])

            pe = dr[:, :, :, NOPE:D]
            nc.vector.tensor_tensor(out=a[:], in0=pe, in1=table(0), op=MULT)
            nc.vector.tensor_tensor(out=pe, in0=pe, in1=table(1), op=MULT)

        def combine(u):
            b, h0, nh, js = UNITS[u]
            j0, nj = js[0], len(js)
            a, dr = st[("a", u)], st[("dr", u)]
            dst = da_of[b][:, j0:j0 + nj, h0 * D:(h0 + nh) * D].rearrange("p j (h d) -> p j h d", d=D)[:, :, :, NOPE:D]
            sw = dr[:, :, :, NOPE:D].rearrange("p j h (f e) -> p j h f e", e=2)[:, :, :, :, ::-1]
            nc.vector.tensor_tensor(out=dst.rearrange("p j h (f e) -> p j h f e", e=2),
                              in0=a[:].rearrange("p j h (f e) -> p j h f e", e=2), in1=sw, op=ADD)

        def tile_of(key, shape, dt, name, bufs):
            if key not in st:
                st[key] = pool.tile(shape, dt, name=name, bufs=bufs, align_bytes=64)
            return st[key]

        def words_of(tile, pat):
            return tile[:].rearrange(pat).bitcast(F32)


        def new_bank(shape, dt, bank):
            return psum.tile(shape, dt, name=bank)

        def turn(eng, out, src):
            if eng == "g":
                nc.gpsimd.tensor_scalar(out=out, in0=src.rearrange("p j w -> p w j"), scalar1=1.0, scalar2=0.0, op0=MULT, op1=ADD)
            else:
                copier[eng](out=out.rearrange("p (c i) j -> p c j i", i=4), in_=src.rearrange("p j (c i) -> p c j i", i=4))

        def interleave(b, w0, w1, eng):
            ti = tile_of(("ti", b, w0), [P, NT, PACK], BF16, "ti", 3)
            turn(eng, ti[:, 0:w1 - w0, :], da_of[b][:, :, w0:w1])

        def token_quant(b, w0, w1):
            ti = st[("ti", b, w0)]
            o = 0
            while o < w1 - w0:
                n = [k for k in (512, 256, 128, 64) if k <= w1 - w0 - o][0]
                c = slice(w0 + o, w0 + o + n)
                nc.vector.quantize_mx(out=tcd[:, b, c].bitcast(E5), scales=tsc[:, b, c], in_=ti[:, o:o + n, :].rearrange("p w j -> p (w j)"))
                o += n

        def slot_turn(j, g0, ng):
            src = da_of[0][:, j, :].bitcast(F32)
            tr = psum.tile([P, 2, 2, P], F32, name="tr", bufs=2)
            for k in range(ng):
                for v in range(2):
                    nc.tensor.transpose(tr[:, k, v, :], src[:, 256 * (g0 + k) + v:256 * (g0 + k + 1):2], ident[:])
            st[("str", j, g0)] = tr

        def slot_copy(j, g0, ng, eng):
            fs = tile_of(("fs", j), [P, NPASS_J, P, PACK], BF16, "fs", 2)
            words = words_of(fs, "p g r t -> p (g r t)")
            copier[eng](out=words[:, 256 * g0:256 * (g0 + ng)].rearrange("p (k r v) -> p k r v", k=ng, v=2),
                        in_=st[("str", j, g0)][:, 0:ng, :, :].rearrange("p k v r -> p k r v"))

        def slot_quant(j):
            fi = st[("fs", j)][:].rearrange("p g r t -> p (g r t)")
            for (lo, n) in ((0, 256), (256, 128)):
                c = slice(j * NPASS_J * P + lo, j * NPASS_J * P + lo + n)
                nc.vector.quantize_mx(out=fc0[:, c].bitcast(E5), scales=fs0[:, c], in_=fi[:, 4 * lo:4 * (lo + n)])

        def feature_turn(g, js):
            tr = psum.tile([P, 2, 2, P], F32, name="tr", bufs=2)
            for k, j in enumerate(js):
                src = da_of[1][:, j, :].bitcast(F32)
                for v in range(2):
                    nc.tensor.transpose(tr[:, k, v, :], src[:, 256 * g + v:256 * (g + 1):2], ident[:])
            st[("tr", g, js)] = tr

        def feature_copy(g, js, eng):
            fi = tile_of(("fi", g), [P, S, PACK], BF16, "fi", 3)
            n = len(js)
            copier[eng](out=words_of(fi, "p n t -> p (n t)")[:, 256 * js[0]:256 * (js[0] + n)].rearrange("p (k r v) -> p k r v", k=n, v=2),
                        in_=st[("tr", g, js)][:, 0:n, :, :].rearrange("p k v r -> p k r v"))

        def feature_quant(g, js):
            c = slice(js[0] * P, (js[0] + len(js)) * P)
            nc.vector.quantize_mx(out=fcd[:, g, c].bitcast(E5), scales=fsc[:, g, c], in_=st[("fi", g)][:, c, :].rearrange("p n t -> p (n t)"))

        def piece_turn(kind, g, n, k, bank):
            raw = raw_of[(kind, g)]
            pb = new_bank([P, 2, NT], BF16, bank)
            st[("pb", kind, g, n, k)] = pb
            for v in range(2):
                c0 = n * NT + (2 * k + v) * P
                nc.tensor.matmul(pb[:, v, :], lhsT=ident_b[:], rhs=raw[:, :, c0:c0 + P].rearrange("p t c -> p c t"), start=True, stop=True)

        def piece_copy(kind, g, n, k, eng):
            s = tile_of(("stage", kind, g, n), [P, NT, PACK], BF16, "stage", 3)
            copier[eng](out=s[:, 256 * k:256 * (k + 1), :].rearrange("p c t -> p (c t)"),
                        in_=st[("pb", kind, g, n, k)][:].rearrange("p v n -> p (v n)"))

        def piece_direct(kind, g, n, k, eng):
            s = tile_of(("stage", kind, g, n), [P, NT, PACK], BF16, "stage", 3)
            turn(eng, s[:, 256 * k:256 * (k + 1), :], raw_of[(kind, g)][:, :, n * NT + 256 * k:n * NT + 256 * (k + 1)])

        def piece_quant(kind, g, n):
            codes, scales = (xc, xs) if kind == "x" else (wc, ws)
            c = slice(n * NT, (n + 1) * NT)
            nc.vector.quantize_mx(out=codes[:, g, c].bitcast(E4), scales=scales[:, g, c], in_=st[("stage", kind, g, n)][:].rearrange("p n t -> p (n t)"))

        def dw_multiply(f, n, bank):
            acc = new_bank([P, NT], F32, bank)
            st[("dw", f, n)] = acc
            r, c = slice(f * P, (f + 1) * P), slice(n * NT, (n + 1) * NT)
            for b in range(B):
                nc.tensor.matmul_mx(out=acc[:], lhsT=tcd[:, b, r].bitcast(E5), lhsT_scale=tsc[:, b, r],
                                    rhs=xc[:, b, c].bitcast(E4), rhs_scale=xs[:, b, c], start=(b == 0), stop=(b == B - 1))

        def dx_codes(b, j, g):
            if b == 0:
                c = slice((j * NPASS_J + g) * P, (j * NPASS_J + g + 1) * P)
                return fc0[:, c], fs0[:, c]
            return fcd[:, g, j * P:(j + 1) * P], fsc[:, g, j * P:(j + 1) * P]

        def dx_multiply(b, j, n, passes, bank=None):
            if passes[0] == 0:
                st[("dx", b, j, n)] = new_bank([P, NT], F32, bank)
            c = slice(n * NT, (n + 1) * NT)
            for g in passes:
                codes, scales = dx_codes(b, j, g)
                nc.tensor.matmul_mx(out=st[("dx", b, j, n)][:], lhsT=codes.bitcast(E5), lhsT_scale=scales,
                                    rhs=wc[:, g, c].bitcast(E4), rhs_scale=ws[:, g, c], start=(g == 0), stop=(g == NPASS_J - 1))

        def leave(key, n, eng, dst):
            if key not in left and len(left) >= 8 and len(left) % 2 == 1:
                st[("o",) + key] = pool.tile([P, DIM], F32, name="raw", bufs=4)
            o = tile_of(("o",) + key, [P, DIM], F32, "o", 4)
            copier[eng](out=o[:, n * NT:(n + 1) * NT], in_=st[key + (n,)][:])
            left[key] = left.get(key, 0) + 1
            if left[key] == 2:
                nc.sync.dma_start(out=dst, in_=o[:])

        left = {}

        def dw_leave(f, n, eng):
            leave(("dw", f), n, eng, out_1[f * P:(f + 1) * P, :])

        def dx_leave(b, j, n, eng):
            leave(("dx", b, j), n, eng, out_0[b].rearrange("(p j) d -> p j d", j=PACK)[:, j, :])

        steps = {"coef": coef, "lift": lift, "plain": plain_part, "prod": products, "comb": combine,
                 "il": interleave, "tq": token_quant, "st": slot_turn, "sc": slot_copy, "sq": slot_quant,
                 "tr": feature_turn, "fc": feature_copy, "fq": feature_quant,
                 "pt": piece_turn, "pc": piece_copy, "pd": piece_direct, "pq": piece_quant,
                 "dw": dw_multiply, "dwl": dw_leave, "dx": dx_multiply, "dxl": dx_leave}

        def run_step(step):
            steps[step[0]](*step[1:])

        for step in PLAN:
            run_step(step)
